import numpy as np
import ml_dtypes


def mxq(x, axis, fmt="e4m3"):
    dtype, down = {"e4m3": (ml_dtypes.float8_e4m3fn, 7), "e5m2": (ml_dtypes.float8_e5m2, 14)}[fmt]
    v = np.moveaxis(np.asarray(x, np.float32).astype(ml_dtypes.bfloat16).astype(np.float64), axis, -1)
    blocks = v.reshape(v.shape[:-1] + (-1, 32))
    amax = np.abs(blocks).max(-1, keepdims=True)
    byte = np.maximum(np.where(amax > 0, np.frexp(amax)[1] - 1 + 127, 0) - down, 1)
    scale = np.exp2(byte - 127.0)
    codes = (blocks / scale).astype(np.float32).astype(dtype).astype(np.float64)
    return np.moveaxis((codes * scale).reshape(v.shape), -1, axis)


WIDE = False


def mx_kscale(k):
    if not WIDE:
        return np.ones(k)
    levels = np.array([10, -10, 5, -5, 0])
    a = np.random.permutation(np.resize(levels, k // 512 * 4)).reshape(k // 512, 4)
    idx = np.arange(k)
    return np.exp2(a[idx // 512, idx % 128 // 32])


BF16 = ml_dtypes.bfloat16


def bf(x):
    return np.asarray(x, np.float32).astype(BF16)


def f64(x):
    return np.asarray(x).astype(np.float64)


B, N, D, H, DH, GD = 2, 1024, 1024, 8, 128, 128
INNER = H * DH


def silu(v):
    return v / (1.0 + np.exp(-v))


def to_heads(t):
    return t.reshape(B, N, H, DH).transpose(0, 2, 1, 3)


def setup_inputs():
    s = mx_kscale(D)
    theta = (10000.0 ** (-2.0 / INNER * np.arange(INNER)) * (1.0 + 0.1 * np.random.standard_normal(INNER))).reshape(H, 1, DH)
    ang = theta * np.arange(N).reshape(1, N, 1)
    return {"x": bf(np.random.standard_normal((B, N, D)) * s),
            "w_k": bf(np.random.standard_normal((D, INNER)) / np.sqrt(D) / s[:, None]),
            "w_v": bf(np.random.standard_normal((D, INNER)) / np.sqrt(D) / s[:, None]),
            "cos_tab": bf(np.cos(ang)), "sin_tab": bf(np.sin(ang))}


def reference(x, w_k, w_v, cos_tab, sin_tab):
    xq = mxq(f64(x), 2, "e4m3")
    k = to_heads(silu(xq @ mxq(f64(w_k), 0, "e4m3")))
    v = to_heads(silu(xq @ mxq(f64(w_v), 0, "e4m3")))
    c, s = f64(cos_tab)[None], f64(sin_tab)[None]
    k_rot = np.concatenate([k * c, k * s], axis=-1) / np.sqrt(2 * DH)
    return mxq(k_rot, 2, "e4m3").transpose(0, 1, 3, 2) @ mxq(v, 2, "e4m3")

@@ -1,0 +1,238 @@
+from contextlib import ExitStack
+
+import concourse.masks as masks
+import concourse.mybir as mybir
+
+BF16 = mybir.dt.bfloat16
+F32 = mybir.dt.float32
+U32 = mybir.dt.uint32
+U8 = mybir.dt.uint8
+FP8X4 = mybir.dt.float8_e4m3fn_x4
+ACT = mybir.ActivationFunctionType
+
+P = 128
+PACK = 4
+K_PASS = P * PACK
+
+B, N, D, H, DH = 2, 1024, 1024, 8, 128
+D_PASSES = D // K_PASS
+N_PASSES = N // K_PASS
+PAIR = 2
+ROUNDS = H // PAIR
+W_COLS = PAIR * DH
+X_AHEAD = 2
+STATE_LAG = 2
+
+FLOPS = 2 * B * N * D * 2 * H * DH + 2 * B * H * 2 * DH * DH * N
+
+
+def tile_linearattention_pa_kernel(tc, x, w_k, w_v, cos_tab, sin_tab, out):
+    nc = tc.nc
+    with ExitStack() as ctx:
+        ctx.enter_context(tc.manual_schedule())
+        once = ctx.enter_context(tc.tile_pool(name="once", bufs=1))
+        twice = ctx.enter_context(tc.tile_pool(name="twice", bufs=2))
+        ring = ctx.enter_context(tc.tile_pool(name="ring", bufs=3))
+        psum_banks = ctx.enter_context(tc.psum_pool(name="psum_banks", bufs=6))
+        psum_state = ctx.enter_context(tc.psum_pool(name="psum_state", bufs=2))
+
+        x_raw = {}
+        w_raw = {}
+        tables = {}
+
+        def load_x(b, g):
+            x_raw[b, g] = once.tile([P, PACK * D], BF16, name="x_raw_%d_%d" % (b, g))
+            rows = x[b, g * K_PASS : (g + 1) * K_PASS, :]
+            nc.sync.dma_start(out=x_raw[b, g][:], in_=rows.rearrange("(p t) d -> p (t d)", t=PACK))
+
+        def load_weights(r):
+            w_raw[r] = once.tile([P, 2, 4, 2, W_COLS], BF16, name="w_raw_%d" % r)
+            cols = slice(r * W_COLS, (r + 1) * W_COLS)
+            for kv, w in enumerate((w_k, w_v)):
+                rows = w.rearrange("(a q e) c -> q a e c", a=4, e=2)
+                for e in range(2):
+                    nc.sync.dma_start(out=w_raw[r][:, kv, :, e, :], in_=rows[:, :, e, cols])
+
+        def load_tables(r):
+            tables[r] = once.tile([P, N_PASSES, PAIR, 2, PACK * DH], BF16, name="tables_%d" % r)
+            heads = slice(r * PAIR, (r + 1) * PAIR)
+            for g in range(N_PASSES):
+                for s, table in enumerate((cos_tab, sin_tab)):
+                    nc.sync.dma_start(
+                        out=tables[r][:, g, :, s, :],
+                        in_=table[heads, g * K_PASS : (g + 1) * K_PASS, :].rearrange(
+                            "h (p t) j -> p h (t j)", t=PACK
+                        ),
+                    )
+
+        load_x(0, 0)
+        load_x(0, 1)
+        load_weights(0)
+        load_tables(0)
+        load_x(1, 0)
+        load_x(1, 1)
+        for r in range(1, ROUNDS):
+            load_weights(r)
+            load_tables(r)
+
+        identity = once.tile([P, P], F32)
+        masks.make_identity(nc, identity[:])
+
+        x_words = {}
+        x_scales = {}
+
+        def quantise_x(b, g):
+            x_f32 = x_raw[b, g][:].bitcast(F32)
+            grouped = twice.tile([P, PACK * D], BF16, name="x_grouped", align_bytes=64)
+            grouped_f32 = grouped[:].bitcast(F32)
+            row = D // 2
+            for t in range(PACK):
+                turned = psum_banks.tile([P, 4, P], F32, name="x_turned", tag="bank")
+                for a in range(4):
+                    nc.tensor.transpose(
+                        turned[:, a, :], x_f32[:, t * row + a * P : t * row + (a + 1) * P], identity[:]
+                    )
+                nc.scalar.copy(
+                    out=grouped_f32[:, t * row : (t + 1) * row].rearrange(
+                        "q (c p u) -> q c p u", c=D_PASSES, u=2
+                    ),
+                    in_=turned[:].rearrange("q (c u) p -> q c p u", u=2),
+                )
+            x_words[b, g] = once.tile([P, D], U32, name="x_words_%d_%d" % (b, g), align_bytes=64)
+            x_scales[b, g] = once.tile([P, D], U8, name="x_scales_%d_%d" % (b, g), align_bytes=64)
+            nc.vector.quantize_mx(
+                out=x_words[b, g][:].bitcast(FP8X4), scales=x_scales[b, g][:], in_=grouped[:]
+            )
+
+        w_words = {}
+        w_scales = {}
+
+        def quantise_weights(r):
+            w_words[r] = twice.tile([P, 2, D_PASSES, W_COLS], U32, name="w_words", align_bytes=64)
+            w_scales[r] = twice.tile([P, 2, D_PASSES, W_COLS], U8, name="w_scales", align_bytes=64)
+            grouped = {}
+            for kv, copy in enumerate((nc.scalar.copy, nc.vector.tensor_copy)):
+                grouped[kv] = once.tile(
+                    [P, D_PASSES, W_COLS * PACK], BF16, name="w_grouped_%d" % kv, align_bytes=64
+                )
+                for c in range(D_PASSES):
+                    copy(
+                        out=grouped[kv][:, c, :].rearrange("q (w i t) -> q w t i", i=4, t=PACK),
+                        in_=w_raw[r][:, kv, 2 * c : 2 * c + 2, :, :].rearrange(
+                            "q u e (w i) -> q w (u e) i", i=4
+                        ),
+                    )
+            for kv in (1, 0):
+                nc.vector.quantize_mx(
+                    out=w_words[r][:, kv, :, :].rearrange("q c w -> q (c w)").bitcast(FP8X4),
+                    scales=w_scales[r][:, kv, :, :].rearrange("q c w -> q (c w)"),
+                    in_=grouped[kv][:].rearrange("q c w -> q (c w)"),
+                )
+
+        def project(r, b, g, kv, hh):
+            bank = psum_banks.tile([P, PACK, DH], F32, name="kv_bank", tag="bank")
+            cols = slice(hh * DH, (hh + 1) * DH)
+            for t in range(PACK):
+                for c in range(D_PASSES):
+                    rows = slice((t * D_PASSES + c) * P, (t * D_PASSES + c + 1) * P)
+                    nc.tensor.matmul_mx(
+                        out=bank[:, t, :],
+                        lhsT=x_words[b, g][:, rows].bitcast(FP8X4),
+                        lhsT_scale=x_scales[b, g][:, rows],
+                        rhs=w_words[r][:, kv, c, cols].bitcast(FP8X4),
+                        rhs_scale=w_scales[r][:, kv, c, cols],
+                        start=(c == 0),
+                        stop=(c == D_PASSES - 1),
+                    )
+            return bank[:].rearrange("p t j -> p j t")
+
+        k_rot = {}
+        v = {}
+
+        def keys_and_values(r, b, g):
+            if g == 0:
+                k_rot[r, b] = twice.tile(
+                    [P, N_PASSES, PAIR, 2, DH * PACK], BF16, name="k_rot", align_bytes=64
+                )
+                v[r, b] = ring.tile([P, N_PASSES, PAIR, DH * PACK], BF16, name="v", align_bytes=64)
+            k = ring.tile([P, PAIR, DH * PACK], F32, name="k")
+            for hh in range(PAIR):
+                nc.scalar.activation(
+                    out=k[:, hh, :].rearrange("p (j t) -> p j t", t=PACK),
+                    in_=project(r, b, g, 0, hh),
+                    func=ACT.Silu,
+                )
+                nc.scalar.activation(
+                    out=v[r, b][:, g, hh, :].rearrange("p (j t) -> p j t", t=PACK),
+                    in_=project(r, b, g, 1, hh),
+                    func=ACT.Silu,
+                )
+            nc.vector.tensor_tensor(
+                out=k_rot[r, b][:, g, :, :, :].rearrange("p h s (j t) -> p h s j t", t=PACK),
+                in0=k[:]
+                .rearrange("p h (j t) -> p h j t", t=PACK)
+                .unsqueeze(2)
+                .to_broadcast([P, PAIR, 2, DH, PACK]),
+                in1=tables[r][:, g, :, :, :].rearrange("p h s (t j) -> p h s j t", t=PACK),
+                op=mybir.AluOpType.mult,
+            )
+
+        k_words = {}
+        k_scales = {}
+        v_words = {}
+        v_scales = {}
+
+        def quantise_keys_and_values(r, b):
+            k_words[r, b] = ring.tile([P, N_PASSES, PAIR, 2, DH], U32, name="k_words", align_bytes=64)
+            k_scales[r, b] = ring.tile([P, N_PASSES, PAIR, 2, DH], U8, name="k_scales", align_bytes=64)
+            v_words[r, b] = ring.tile([P, N_PASSES, PAIR, DH], U32, name="v_words", align_bytes=64)
+            v_scales[r, b] = ring.tile([P, N_PASSES, PAIR, DH], U8, name="v_scales", align_bytes=64)
+            nc.vector.quantize_mx(
+                out=v_words[r, b][:].rearrange("p g h j -> p (g h j)").bitcast(FP8X4),
+                scales=v_scales[r, b][:].rearrange("p g h j -> p (g h j)"),
+                in_=v[r, b][:].rearrange("p g h w -> p (g h w)"),
+            )
+            nc.vector.quantize_mx(
+                out=k_words[r, b][:].rearrange("p g h s j -> p (g h s j)").bitcast(FP8X4),
+                scales=k_scales[r, b][:].rearrange("p g h s j -> p (g h s j)"),
+                in_=k_rot[r, b][:].rearrange("p g h s w -> p (g h s w)"),
+            )
+
+        def state(r, b):
+            sums = psum_state.tile([P, PAIR, 2, DH], F32, name="sums")
+            for hh in range(PAIR):
+                for s in range(2):
+                    for g in range(N_PASSES):
+                        nc.tensor.matmul_mx(
+                            out=sums[:, hh, s, :],
+                            lhsT=k_words[r, b][:, g, hh, s, :].bitcast(FP8X4),
+                            lhsT_scale=k_scales[r, b][:, g, hh, s, :],
+                            rhs=v_words[r, b][:, g, hh, :].bitcast(FP8X4),
+                            rhs_scale=v_scales[r, b][:, g, hh, :],
+                            start=(g == 0),
+                            stop=(g == N_PASSES - 1),
+                        )
+            result = twice.tile([P, PAIR, 2, DH], F32, name="result")
+            nc.scalar.activation(out=result[:], in_=sums[:], func=ACT.Copy, scale=1.0 / 16.0)
+            nc.sync.dma_start(
+                out=out[b, r * PAIR : (r + 1) * PAIR].rearrange("h (s e) d -> e (h s) d", s=2),
+                in_=result[:].rearrange("e h s d -> e (h s) d"),
+            )
+
+        steps = [(r, b, g) for r in range(ROUNDS) for b in range(B) for g in range(N_PASSES)]
+        chunks = [(b, g) for b in range(B) for g in range(N_PASSES)]
+        for b, g in chunks[:X_AHEAD]:
+            quantise_x(b, g)
+        quantise_weights(0)
+        for i in range(len(steps) + STATE_LAG):
+            if i < len(steps):
+                r, b, g = steps[i]
+                keys_and_values(r, b, g)
+                if i + X_AHEAD < len(chunks):
+                    quantise_x(*chunks[i + X_AHEAD])
+                if (b, g) == (1, 0) and r + 1 < ROUNDS:
+                    quantise_weights(r + 1)
+                if g == N_PASSES - 1:
+                    quantise_keys_and_values(r, b)
+            if i >= STATE_LAG and steps[i - STATE_LAG][2] == N_PASSES - 1:
+                state(*steps[i - STATE_LAG][:2])

@@ -20,8 +20,7 @@ N_PASSES = N // K_PASS
 PAIR = 2
 ROUNDS = H // PAIR
 W_COLS = PAIR * DH
-X_AHEAD = 2
-STATE_LAG = 2
+KEYS, VALUES = 0, 1
 
 FLOPS = 2 * B * N * D * 2 * H * DH + 2 * B * H * 2 * DH * DH * N
 
@@ -32,7 +31,8 @@ def tile_linearattention_pa_kernel(tc, x, w_k, w_v, cos_tab, sin_tab, out):
         ctx.enter_context(tc.manual_schedule())
         once = ctx.enter_context(tc.tile_pool(name="once", bufs=1))
         twice = ctx.enter_context(tc.tile_pool(name="twice", bufs=2))
-        ring = ctx.enter_context(tc.tile_pool(name="ring", bufs=3))
+        thrice = ctx.enter_context(tc.tile_pool(name="thrice", bufs=3))
+        four = ctx.enter_context(tc.tile_pool(name="four", bufs=4))
         psum_banks = ctx.enter_context(tc.psum_pool(name="psum_banks", bufs=6))
         psum_state = ctx.enter_context(tc.psum_pool(name="psum_state", bufs=2))
 
@@ -41,39 +41,42 @@ def tile_linearattention_pa_kernel(tc, x, w_k, w_v, cos_tab, sin_tab, out):
         tables = {}
 
         def load_x(b, g):
-            x_raw[b, g] = once.tile([P, PACK * D], BF16, name="x_raw_%d_%d" % (b, g))
-            rows = x[b, g * K_PASS : (g + 1) * K_PASS, :]
-            nc.sync.dma_start(out=x_raw[b, g][:], in_=rows.rearrange("(p t) d -> p (t d)", t=PACK))
+            rows = x[b, g * K_PASS : (g + 1) * K_PASS, :].rearrange("(p t) d -> p t d", t=PACK)
+            for t in range(PACK):
+                x_raw[b, g, t] = once.tile([P, D], BF16, name="x_raw_%d_%d_%d" % (b, g, t))
+                nc.sync.dma_start(out=x_raw[b, g, t][:], in_=rows[:, t, :])
 
-        def load_weights(r):
-            w_raw[r] = once.tile([P, 2, 4, 2, W_COLS], BF16, name="w_raw_%d" % r)
-            cols = slice(r * W_COLS, (r + 1) * W_COLS)
-            for kv, w in enumerate((w_k, w_v)):
-                rows = w.rearrange("(a q e) c -> q a e c", a=4, e=2)
-                for e in range(2):
-                    nc.sync.dma_start(out=w_raw[r][:, kv, :, e, :], in_=rows[:, :, e, cols])
+        def load_weights(r, kv):
+            w_raw[r, kv] = once.tile([P, 4, 2, W_COLS], BF16, name="w_raw_%d_%d" % (r, kv))
+            rows = (w_k, w_v)[kv].rearrange("(a q e) c -> q a e c", a=4, e=2)
+            for e in range(2):
+                nc.sync.dma_start(
+                    out=w_raw[r, kv][:, :, e, :], in_=rows[:, :, e, r * W_COLS : (r + 1) * W_COLS]
+                )
 
-        def load_tables(r):
-            tables[r] = once.tile([P, N_PASSES, PAIR, 2, PACK * DH], BF16, name="tables_%d" % r)
-            heads = slice(r * PAIR, (r + 1) * PAIR)
-            for g in range(N_PASSES):
-                for s, table in enumerate((cos_tab, sin_tab)):
-                    nc.sync.dma_start(
-                        out=tables[r][:, g, :, s, :],
-                        in_=table[heads, g * K_PASS : (g + 1) * K_PASS, :].rearrange(
-                            "h (p t) j -> p h (t j)", t=PACK
-                        ),
-                    )
+        def load_tables(r, g):
+            tables[r, g] = once.tile([P, PAIR, 2, PACK * DH], BF16, name="tables_%d_%d" % (r, g))
+            for s, table in enumerate((cos_tab, sin_tab)):
+                nc.sync.dma_start(
+                    out=tables[r, g][:, :, s, :],
+                    in_=table[r * PAIR : (r + 1) * PAIR, g * K_PASS : (g + 1) * K_PASS, :].rearrange(
+                        "h (p t) j -> p h (t j)", t=PACK
+                    ),
+                )
 
+        load_weights(0, KEYS)
         load_x(0, 0)
+        load_tables(0, 0)
         load_x(0, 1)
-        load_weights(0)
-        load_tables(0)
+        load_tables(0, 1)
+        load_weights(0, VALUES)
         load_x(1, 0)
         load_x(1, 1)
         for r in range(1, ROUNDS):
-            load_weights(r)
-            load_tables(r)
+            load_weights(r, KEYS)
+            load_tables(r, 0)
+            load_tables(r, 1)
+            load_weights(r, VALUES)
 
         identity = once.tile([P, P], F32)
         masks.make_identity(nc, identity[:])
@@ -82,100 +85,94 @@ def tile_linearattention_pa_kernel(tc, x, w_k, w_v, cos_tab, sin_tab, out):
         x_scales = {}
 
         def quantise_x(b, g):
-            x_f32 = x_raw[b, g][:].bitcast(F32)
-            grouped = twice.tile([P, PACK * D], BF16, name="x_grouped", align_bytes=64)
-            grouped_f32 = grouped[:].bitcast(F32)
-            row = D // 2
+            x_words[b, g] = once.tile([P, PACK, D_PASSES, P], U32, name="x_words_%d_%d" % (b, g), align_bytes=64)
+            x_scales[b, g] = once.tile([P, PACK, D_PASSES, P], U8, name="x_scales_%d_%d" % (b, g), align_bytes=64)
             for t in range(PACK):
+                x_f32 = x_raw[b, g, t][:].bitcast(F32)
                 turned = psum_banks.tile([P, 4, P], F32, name="x_turned", tag="bank")
                 for a in range(4):
-                    nc.tensor.transpose(
-                        turned[:, a, :], x_f32[:, t * row + a * P : t * row + (a + 1) * P], identity[:]
-                    )
+                    nc.tensor.transpose(turned[:, a, :], x_f32[:, a * P : (a + 1) * P], identity[:])
+                grouped = four.tile([P, D], BF16, name="x_grouped", align_bytes=64)
                 nc.scalar.copy(
-                    out=grouped_f32[:, t * row : (t + 1) * row].rearrange(
-                        "q (c p u) -> q c p u", c=D_PASSES, u=2
-                    ),
+                    out=grouped[:].bitcast(F32).rearrange("q (c p u) -> q c p u", c=D_PASSES, u=2),
                     in_=turned[:].rearrange("q (c u) p -> q c p u", u=2),
                 )
-            x_words[b, g] = once.tile([P, D], U32, name="x_words_%d_%d" % (b, g), align_bytes=64)
-            x_scales[b, g] = once.tile([P, D], U8, name="x_scales_%d_%d" % (b, g), align_bytes=64)
-            nc.vector.quantize_mx(
-                out=x_words[b, g][:].bitcast(FP8X4), scales=x_scales[b, g][:], in_=grouped[:]
-            )
+                nc.vector.quantize_mx(
+                    out=x_words[b, g][:, t, :, :].rearrange("q c p -> q (c p)").bitcast(FP8X4),
+                    scales=x_scales[b, g][:, t, :, :].rearrange("q c p -> q (c p)"),
+                    in_=grouped[:],
+                )
 
         w_words = {}
         w_scales = {}
 
-        def quantise_weights(r):
-            w_words[r] = twice.tile([P, 2, D_PASSES, W_COLS], U32, name="w_words", align_bytes=64)
-            w_scales[r] = twice.tile([P, 2, D_PASSES, W_COLS], U8, name="w_scales", align_bytes=64)
-            grouped = {}
-            for kv, copy in enumerate((nc.scalar.copy, nc.vector.tensor_copy)):
-                grouped[kv] = once.tile(
-                    [P, D_PASSES, W_COLS * PACK], BF16, name="w_grouped_%d" % kv, align_bytes=64
+        def quantise_weights(r, kv):
+            copy = (nc.vector.tensor_copy, nc.scalar.copy)[kv]
+            grouped = twice.tile([P, D_PASSES, W_COLS * PACK], BF16, name="w_grouped_%d" % kv, align_bytes=64)
+            for c in range(D_PASSES):
+                copy(
+                    out=grouped[:, c, :].rearrange("q (w i t) -> q w t i", i=4, t=PACK),
+                    in_=w_raw[r, kv][:, 2 * c : 2 * c + 2, :, :].rearrange("q u e (w i) -> q w (u e) i", i=4),
                 )
-                for c in range(D_PASSES):
-                    copy(
-                        out=grouped[kv][:, c, :].rearrange("q (w i t) -> q w t i", i=4, t=PACK),
-                        in_=w_raw[r][:, kv, 2 * c : 2 * c + 2, :, :].rearrange(
-                            "q u e (w i) -> q w (u e) i", i=4
-                        ),
-                    )
-            for kv in (1, 0):
-                nc.vector.quantize_mx(
-                    out=w_words[r][:, kv, :, :].rearrange("q c w -> q (c w)").bitcast(FP8X4),
-                    scales=w_scales[r][:, kv, :, :].rearrange("q c w -> q (c w)"),
-                    in_=grouped[kv][:].rearrange("q c w -> q (c w)"),
-                )
+            w_words[r, kv] = twice.tile([P, D_PASSES, W_COLS], U32, name="w_words_%d" % kv, align_bytes=64)
+            w_scales[r, kv] = twice.tile([P, D_PASSES, W_COLS], U8, name="w_scales_%d" % kv, align_bytes=64)
+            nc.vector.quantize_mx(
+                out=w_words[r, kv][:].rearrange("q c w -> q (c w)").bitcast(FP8X4),
+                scales=w_scales[r, kv][:].rearrange("q c w -> q (c w)"),
+                in_=grouped[:].rearrange("q c w -> q (c w)"),
+            )
 
         def project(r, b, g, kv, hh):
             bank = psum_banks.tile([P, PACK, DH], F32, name="kv_bank", tag="bank")
             cols = slice(hh * DH, (hh + 1) * DH)
             for t in range(PACK):
                 for c in range(D_PASSES):
-                    rows = slice((t * D_PASSES + c) * P, (t * D_PASSES + c + 1) * P)
                     nc.tensor.matmul_mx(
                         out=bank[:, t, :],
-                        lhsT=x_words[b, g][:, rows].bitcast(FP8X4),
-                        lhsT_scale=x_scales[b, g][:, rows],
-                        rhs=w_words[r][:, kv, c, cols].bitcast(FP8X4),
-                        rhs_scale=w_scales[r][:, kv, c, cols],
+                        lhsT=x_words[b, g][:, t, c, :].bitcast(FP8X4),
+                        lhsT_scale=x_scales[b, g][:, t, c, :],
+                        rhs=w_words[r, kv][:, c, cols].bitcast(FP8X4),
+                        rhs_scale=w_scales[r, kv][:, c, cols],
                         start=(c == 0),
                         stop=(c == D_PASSES - 1),
                     )
             return bank[:].rearrange("p t j -> p j t")
 
+        k = {}
         k_rot = {}
         v = {}
 
-        def keys_and_values(r, b, g):
-            if g == 0:
-                k_rot[r, b] = twice.tile(
-                    [P, N_PASSES, PAIR, 2, DH * PACK], BF16, name="k_rot", align_bytes=64
-                )
-                v[r, b] = ring.tile([P, N_PASSES, PAIR, DH * PACK], BF16, name="v", align_bytes=64)
-            k = ring.tile([P, PAIR, DH * PACK], F32, name="k")
+        def project_keys(r, b, g):
+            k[r, b, g] = four.tile([P, PAIR, DH * PACK], F32, name="k")
             for hh in range(PAIR):
                 nc.scalar.activation(
-                    out=k[:, hh, :].rearrange("p (j t) -> p j t", t=PACK),
-                    in_=project(r, b, g, 0, hh),
+                    out=k[r, b, g][:, hh, :].rearrange("p (j t) -> p j t", t=PACK),
+                    in_=project(r, b, g, KEYS, hh),
                     func=ACT.Silu,
                 )
-                nc.scalar.activation(
-                    out=v[r, b][:, g, hh, :].rearrange("p (j t) -> p j t", t=PACK),
-                    in_=project(r, b, g, 1, hh),
-                    func=ACT.Silu,
-                )
+
+        def rotate_keys(r, b, g):
+            if g == 0:
+                k_rot[r, b] = twice.tile([P, N_PASSES, PAIR, 2, DH * PACK], BF16, name="k_rot", align_bytes=64)
             nc.vector.tensor_tensor(
                 out=k_rot[r, b][:, g, :, :, :].rearrange("p h s (j t) -> p h s j t", t=PACK),
-                in0=k[:]
+                in0=k[r, b, g][:]
                 .rearrange("p h (j t) -> p h j t", t=PACK)
                 .unsqueeze(2)
                 .to_broadcast([P, PAIR, 2, DH, PACK]),
-                in1=tables[r][:, g, :, :, :].rearrange("p h s (t j) -> p h s j t", t=PACK),
+                in1=tables[r, g][:].rearrange("p h s (t j) -> p h s j t", t=PACK),
                 op=mybir.AluOpType.mult,
             )
+
+        def values(r, b, g):
+            if g == 0:
+                v[r, b] = thrice.tile([P, N_PASSES, PAIR, DH * PACK], BF16, name="v", align_bytes=64)
+            for hh in range(PAIR):
+                nc.scalar.activation(
+                    out=v[r, b][:, g, hh, :].rearrange("p (j t) -> p j t", t=PACK),
+                    in_=project(r, b, g, VALUES, hh),
+                    func=ACT.Silu,
+                )
 
         k_words = {}
         k_scales = {}
@@ -183,19 +180,19 @@ def tile_linearattention_pa_kernel(tc, x, w_k, w_v, cos_tab, sin_tab, out):
         v_scales = {}
 
         def quantise_keys_and_values(r, b):
-            k_words[r, b] = ring.tile([P, N_PASSES, PAIR, 2, DH], U32, name="k_words", align_bytes=64)
-            k_scales[r, b] = ring.tile([P, N_PASSES, PAIR, 2, DH], U8, name="k_scales", align_bytes=64)
-            v_words[r, b] = ring.tile([P, N_PASSES, PAIR, DH], U32, name="v_words", align_bytes=64)
-            v_scales[r, b] = ring.tile([P, N_PASSES, PAIR, DH], U8, name="v_scales", align_bytes=64)
-            nc.vector.quantize_mx(
-                out=v_words[r, b][:].rearrange("p g h j -> p (g h j)").bitcast(FP8X4),
-                scales=v_scales[r, b][:].rearrange("p g h j -> p (g h j)"),
-                in_=v[r, b][:].rearrange("p g h w -> p (g h w)"),
-            )
+            k_words[r, b] = thrice.tile([P, N_PASSES, PAIR, 2, DH], U32, name="k_words", align_bytes=64)
+            k_scales[r, b] = thrice.tile([P, N_PASSES, PAIR, 2, DH], U8, name="k_scales", align_bytes=64)
+            v_words[r, b] = thrice.tile([P, N_PASSES, PAIR, DH], U32, name="v_words", align_bytes=64)
+            v_scales[r, b] = thrice.tile([P, N_PASSES, PAIR, DH], U8, name="v_scales", align_bytes=64)
             nc.vector.quantize_mx(
                 out=k_words[r, b][:].rearrange("p g h s j -> p (g h s j)").bitcast(FP8X4),
                 scales=k_scales[r, b][:].rearrange("p g h s j -> p (g h s j)"),
                 in_=k_rot[r, b][:].rearrange("p g h s w -> p (g h s w)"),
+            )
+            nc.vector.quantize_mx(
+                out=v_words[r, b][:].rearrange("p g h j -> p (g h j)").bitcast(FP8X4),
+                scales=v_scales[r, b][:].rearrange("p g h j -> p (g h j)"),
+                in_=v[r, b][:].rearrange("p g h w -> p (g h w)"),
             )
 
         def state(r, b):
@@ -219,20 +216,32 @@ def tile_linearattention_pa_kernel(tc, x, w_k, w_v, cos_tab, sin_tab, out):
                 in_=result[:].rearrange("e h s d -> e (h s) d"),
             )
 
-        steps = [(r, b, g) for r in range(ROUNDS) for b in range(B) for g in range(N_PASSES)]
-        chunks = [(b, g) for b in range(B) for g in range(N_PASSES)]
-        for b, g in chunks[:X_AHEAD]:
-            quantise_x(b, g)
-        quantise_weights(0)
-        for i in range(len(steps) + STATE_LAG):
-            if i < len(steps):
-                r, b, g = steps[i]
-                keys_and_values(r, b, g)
-                if i + X_AHEAD < len(chunks):
-                    quantise_x(*chunks[i + X_AHEAD])
-                if (b, g) == (1, 0) and r + 1 < ROUNDS:
-                    quantise_weights(r + 1)
-                if g == N_PASSES - 1:
-                    quantise_keys_and_values(r, b)
-            if i >= STATE_LAG and steps[i - STATE_LAG][2] == N_PASSES - 1:
-                state(*steps[i - STATE_LAG][:2])
+        def want_x(b, g):
+            if (b, g) not in x_words:
+                quantise_x(b, g)
+
+        def want_weights(r, kv):
+            if (r, kv) not in w_words:
+                quantise_weights(r, kv)
+
+        units = [(r, b) for r in range(ROUNDS) for b in range(B)]
+        for i, (r, b) in enumerate(units):
+            next_r, next_b = units[min(i + 1, len(units) - 1)]
+            want_weights(r, KEYS)
+            want_x(b, 0)
+            project_keys(r, b, 0)
+            want_x(b, 1)
+            rotate_keys(r, b, 0)
+            project_keys(r, b, 1)
+            want_weights(r, VALUES)
+            rotate_keys(r, b, 1)
+            want_weights(next_r, KEYS)
+            want_x(next_b, 0)
+            values(r, b, 0)
+            want_x(next_b, 1)
+            want_weights(next_r, VALUES)
+            values(r, b, 1)
+            quantise_keys_and_values(r, b)
+            if i > 0:
+                state(*units[i - 1])
+        state(*units[-1])

@@ -21,6 +21,7 @@ PAIR = 2
 ROUNDS = H // PAIR
 W_COLS = PAIR * DH
 KEYS, VALUES = 0, 1
+STATE_LAG = 2
 
 FLOPS = 2 * B * N * D * 2 * H * DH + 2 * B * H * 2 * DH * DH * N
 
@@ -179,16 +180,18 @@ def tile_linearattention_pa_kernel(tc, x, w_k, w_v, cos_tab, sin_tab, out):
         v_words = {}
         v_scales = {}
 
-        def quantise_keys_and_values(r, b):
+        def quantise_keys(r, b):
             k_words[r, b] = thrice.tile([P, N_PASSES, PAIR, 2, DH], U32, name="k_words", align_bytes=64)
             k_scales[r, b] = thrice.tile([P, N_PASSES, PAIR, 2, DH], U8, name="k_scales", align_bytes=64)
-            v_words[r, b] = thrice.tile([P, N_PASSES, PAIR, DH], U32, name="v_words", align_bytes=64)
-            v_scales[r, b] = thrice.tile([P, N_PASSES, PAIR, DH], U8, name="v_scales", align_bytes=64)
             nc.vector.quantize_mx(
                 out=k_words[r, b][:].rearrange("p g h s j -> p (g h s j)").bitcast(FP8X4),
                 scales=k_scales[r, b][:].rearrange("p g h s j -> p (g h s j)"),
                 in_=k_rot[r, b][:].rearrange("p g h s w -> p (g h s w)"),
             )
+
+        def quantise_values(r, b):
+            v_words[r, b] = thrice.tile([P, N_PASSES, PAIR, DH], U32, name="v_words", align_bytes=64)
+            v_scales[r, b] = thrice.tile([P, N_PASSES, PAIR, DH], U8, name="v_scales", align_bytes=64)
             nc.vector.quantize_mx(
                 out=v_words[r, b][:].rearrange("p g h j -> p (g h j)").bitcast(FP8X4),
                 scales=v_scales[r, b][:].rearrange("p g h j -> p (g h j)"),
@@ -225,23 +228,25 @@ def tile_linearattention_pa_kernel(tc, x, w_k, w_v, cos_tab, sin_tab, out):
                 quantise_weights(r, kv)
 
         units = [(r, b) for r in range(ROUNDS) for b in range(B)]
+        chunks = [(b, g) for b in range(B) for g in range(N_PASSES)]
+        want_weights(0, KEYS)
+        want_x(0, 0)
         for i, (r, b) in enumerate(units):
-            next_r, next_b = units[min(i + 1, len(units) - 1)]
-            want_weights(r, KEYS)
-            want_x(b, 0)
-            project_keys(r, b, 0)
-            want_x(b, 1)
-            rotate_keys(r, b, 0)
-            project_keys(r, b, 1)
-            want_weights(r, VALUES)
-            rotate_keys(r, b, 1)
-            want_weights(next_r, KEYS)
-            want_x(next_b, 0)
-            values(r, b, 0)
-            want_x(next_b, 1)
-            want_weights(next_r, VALUES)
-            values(r, b, 1)
-            quantise_keys_and_values(r, b)
-            if i > 0:
-                state(*units[i - 1])
-        state(*units[-1])
+            next_round = min(r + 1, ROUNDS - 1)
+            for g in range(N_PASSES):
+                want_x(*chunks[min(chunks.index((b, g)) + 1, len(chunks) - 1)])
+                if (b, g) == (0, 1):
+                    want_weights(next_round, KEYS)
+                project_keys(r, b, g)
+                rotate_keys(r, b, g)
+                want_weights(r, VALUES)
+                if (b, g) == (1, 0):
+                    want_weights(next_round, VALUES)
+            quantise_keys(r, b)
+            for g in range(N_PASSES):
+                values(r, b, g)
+            quantise_values(r, b)
+            if i >= STATE_LAG:
+                state(*units[i - STATE_LAG])
+        for r, b in units[-STATE_LAG:]:
+            state(r, b)

@@ -21,6 +21,7 @@ PAIR = 2
 ROUNDS = H // PAIR
 W_COLS = PAIR * DH
 KEYS, VALUES = 0, 1
+RUN = 4
 STATE_LAG = 2
 
 FLOPS = 2 * B * N * D * 2 * H * DH + 2 * B * H * 2 * DH * DH * N
@@ -137,7 +138,7 @@ def tile_linearattention_pa_kernel(tc, x, w_k, w_v, cos_tab, sin_tab, out):
                         start=(c == 0),
                         stop=(c == D_PASSES - 1),
                     )
-            return bank[:].rearrange("p t j -> p j t")
+            return bank[:]
 
         k = {}
         k_rot = {}
@@ -147,23 +148,22 @@ def tile_linearattention_pa_kernel(tc, x, w_k, w_v, cos_tab, sin_tab, out):
             k[r, b, g] = four.tile([P, PAIR, DH * PACK], F32, name="k")
             for hh in range(PAIR):
                 nc.scalar.activation(
-                    out=k[r, b, g][:, hh, :].rearrange("p (j t) -> p j t", t=PACK),
-                    in_=project(r, b, g, KEYS, hh),
+                    out=k[r, b, g][:, hh, :].rearrange("p (w t i) -> p w t i", t=PACK, i=RUN),
+                    in_=project(r, b, g, KEYS, hh).rearrange("p t (w i) -> p w t i", i=RUN),
                     func=ACT.Silu,
                 )
 
         def rotate_keys(r, b, g):
             if g == 0:
                 k_rot[r, b] = twice.tile([P, N_PASSES, PAIR, 2, DH * PACK], BF16, name="k_rot", align_bytes=64)
-            nc.vector.tensor_tensor(
-                out=k_rot[r, b][:, g, :, :, :].rearrange("p h s (j t) -> p h s j t", t=PACK),
-                in0=k[r, b, g][:]
-                .rearrange("p h (j t) -> p h j t", t=PACK)
-                .unsqueeze(2)
-                .to_broadcast([P, PAIR, 2, DH, PACK]),
-                in1=tables[r, g][:].rearrange("p h s (t j) -> p h s j t", t=PACK),
-                op=mybir.AluOpType.mult,
-            )
+            for hh in range(PAIR):
+                for s in range(2):
+                    nc.vector.tensor_tensor(
+                        out=k_rot[r, b][:, g, hh, s, :].rearrange("p (w i t) -> p w t i", t=PACK, i=RUN),
+                        in0=k[r, b, g][:, hh, :].rearrange("p (w t i) -> p w t i", t=PACK, i=RUN),
+                        in1=tables[r, g][:, hh, s, :].rearrange("p (t w i) -> p w t i", t=PACK, i=RUN),
+                        op=mybir.AluOpType.mult,
+                    )
 
         def values(r, b, g):
             if g == 0:
@@ -171,7 +171,7 @@ def tile_linearattention_pa_kernel(tc, x, w_k, w_v, cos_tab, sin_tab, out):
             for hh in range(PAIR):
                 nc.scalar.activation(
                     out=v[r, b][:, g, hh, :].rearrange("p (j t) -> p j t", t=PACK),
-                    in_=project(r, b, g, VALUES, hh),
+                    in_=project(r, b, g, VALUES, hh).rearrange("p t j -> p j t"),
                     func=ACT.Silu,
                 )
 

@@ -68,17 +68,24 @@ def tile_linearattention_pa_kernel(tc, x, w_k, w_v, cos_tab, sin_tab, out):
 
         load_weights(0, KEYS)
         load_x(0, 0)
+        load_weights(0, VALUES)
         load_tables(0, 0)
+        load_weights(1, KEYS)
         load_x(0, 1)
         load_tables(0, 1)
-        load_weights(0, VALUES)
         load_x(1, 0)
         load_x(1, 1)
         for r in range(1, ROUNDS):
-            load_weights(r, KEYS)
+            if r > 1:
+                load_weights(r, KEYS)
             load_tables(r, 0)
             load_tables(r, 1)
             load_weights(r, VALUES)
+
+        table_in = once.tile([P, 1], F32)
+        table_out = once.tile([P, 1], F32)
+        nc.vector.memset(table_in[:], 0.0)
+        nc.scalar.activation(out=table_out[:], in_=table_in[:], func=ACT.Silu)
 
         identity = once.tile([P, P], F32)
         masks.make_identity(nc, identity[:])
@@ -89,39 +96,53 @@ def tile_linearattention_pa_kernel(tc, x, w_k, w_v, cos_tab, sin_tab, out):
         def quantise_x(b, g):
             x_words[b, g] = once.tile([P, PACK, D_PASSES, P], U32, name="x_words_%d_%d" % (b, g), align_bytes=64)
             x_scales[b, g] = once.tile([P, PACK, D_PASSES, P], U8, name="x_scales_%d_%d" % (b, g), align_bytes=64)
+            grouped = {}
             for t in range(PACK):
                 x_f32 = x_raw[b, g, t][:].bitcast(F32)
                 turned = psum_banks.tile([P, 4, P], F32, name="x_turned", tag="bank")
                 for a in range(4):
                     nc.tensor.transpose(turned[:, a, :], x_f32[:, a * P : (a + 1) * P], identity[:])
-                grouped = four.tile([P, D], BF16, name="x_grouped", align_bytes=64)
-                nc.scalar.copy(
-                    out=grouped[:].bitcast(F32).rearrange("q (c p u) -> q c p u", c=D_PASSES, u=2),
+                grouped[t] = four.tile([P, D], BF16, name="x_grouped", align_bytes=64)
+                copy = nc.vector.tensor_copy if (b, g) == (0, 0) and t % 2 == 1 else nc.scalar.copy
+                copy(
+                    out=grouped[t][:].bitcast(F32).rearrange("q (c p u) -> q c p u", c=D_PASSES, u=2),
                     in_=turned[:].rearrange("q (c u) p -> q c p u", u=2),
                 )
-                nc.vector.quantize_mx(
-                    out=x_words[b, g][:, t, :, :].rearrange("q c p -> q (c p)").bitcast(FP8X4),
-                    scales=x_scales[b, g][:, t, :, :].rearrange("q c p -> q (c p)"),
-                    in_=grouped[:],
-                )
+                if t > 0:
+                    x_codes(b, g, t - 1, grouped[t - 1])
+            x_codes(b, g, PACK - 1, grouped[PACK - 1])
+
+        def x_codes(b, g, t, grouped):
+            nc.vector.quantize_mx(
+                out=x_words[b, g][:, t, :, :].rearrange("q c p -> q (c p)").bitcast(FP8X4),
+                scales=x_scales[b, g][:, t, :, :].rearrange("q c p -> q (c p)"),
+                in_=grouped[:],
+            )
 
         w_words = {}
         w_scales = {}
 
-        def quantise_weights(r, kv):
-            copy = (nc.vector.tensor_copy, nc.scalar.copy)[kv]
-            grouped = twice.tile([P, D_PASSES, W_COLS * PACK], BF16, name="w_grouped_%d" % kv, align_bytes=64)
+        w_grouped = {}
+
+        def group_weights(r, kv):
+            vector, scalar = nc.vector.tensor_copy, nc.scalar.copy
+            copies = {(0, KEYS): (vector, scalar), (0, VALUES): (vector, vector), (1, KEYS): (vector, vector)}.get(
+                (r, kv), (scalar, scalar)
+            )
+            w_grouped[r, kv] = twice.tile([P, D_PASSES, W_COLS * PACK], BF16, name="w_grouped_%d" % kv, align_bytes=64)
             for c in range(D_PASSES):
-                copy(
-                    out=grouped[:, c, :].rearrange("q (w i t) -> q w t i", i=4, t=PACK),
+                copies[c](
+                    out=w_grouped[r, kv][:, c, :].rearrange("q (w i t) -> q w t i", i=4, t=PACK),
                     in_=w_raw[r, kv][:, 2 * c : 2 * c + 2, :, :].rearrange("q u e (w i) -> q w (u e) i", i=4),
                 )
+
+        def quantise_weights(r, kv):
             w_words[r, kv] = twice.tile([P, D_PASSES, W_COLS], U32, name="w_words_%d" % kv, align_bytes=64)
             w_scales[r, kv] = twice.tile([P, D_PASSES, W_COLS], U8, name="w_scales_%d" % kv, align_bytes=64)
             nc.vector.quantize_mx(
                 out=w_words[r, kv][:].rearrange("q c w -> q (c w)").bitcast(FP8X4),
                 scales=w_scales[r, kv][:].rearrange("q c w -> q (c w)"),
-                in_=grouped[:].rearrange("q c w -> q (c w)"),
+                in_=w_grouped[r, kv][:].rearrange("q c w -> q (c w)"),
             )
 
         def project(r, b, g, kv, hh):
@@ -225,6 +246,8 @@ def tile_linearattention_pa_kernel(tc, x, w_k, w_v, cos_tab, sin_tab, out):
 
         def want_weights(r, kv):
             if (r, kv) not in w_words:
+                if (r, kv) not in w_grouped:
+                    group_weights(r, kv)
                 quantise_weights(r, kv)
 
         units = [(r, b) for r in range(ROUNDS) for b in range(B)]
@@ -234,12 +257,19 @@ def tile_linearattention_pa_kernel(tc, x, w_k, w_v, cos_tab, sin_tab, out):
         for i, (r, b) in enumerate(units):
             next_round = min(r + 1, ROUNDS - 1)
             for g in range(N_PASSES):
-                want_x(*chunks[min(chunks.index((b, g)) + 1, len(chunks) - 1)])
+                if i > 0 or g > 0:
+                    want_x(*chunks[min(chunks.index((b, g)) + 1, len(chunks) - 1)])
+                else:
+                    group_weights(0, VALUES)
                 if (b, g) == (0, 1):
                     want_weights(next_round, KEYS)
                 project_keys(r, b, g)
                 rotate_keys(r, b, g)
                 want_weights(r, VALUES)
+                if i == 0 and g == 0:
+                    group_weights(1, KEYS)
+                    want_x(0, 1)
+                    quantise_weights(1, KEYS)
                 if (b, g) == (1, 0):
                     want_weights(next_round, VALUES)
             quantise_keys(r, b)

@@ -44,9 +44,13 @@ def tile_linearattention_pa_kernel(tc, x, w_k, w_v, cos_tab, sin_tab, out):
 
         def load_x(b, g):
             rows = x[b, g * K_PASS : (g + 1) * K_PASS, :].rearrange("(p t) d -> p t d", t=PACK)
-            for t in range(PACK):
-                x_raw[b, g, t] = once.tile([P, D], BF16, name="x_raw_%d_%d_%d" % (b, g, t))
-                nc.sync.dma_start(out=x_raw[b, g, t][:], in_=rows[:, t, :])
+            for u in range(2):
+                x_raw[b, g, u] = once.tile([P, 2, D], BF16, name="x_raw_%d_%d_%d" % (b, g, u))
+                if (b, g) == (0, 0):
+                    for t in range(2):
+                        nc.sync.dma_start(out=x_raw[b, g, u][:, t, :], in_=rows[:, 2 * u + t, :])
+                else:
+                    nc.sync.dma_start(out=x_raw[b, g, u][:], in_=rows[:, 2 * u : 2 * u + 2, :])
 
         def load_weights(r, kv):
             w_raw[r, kv] = once.tile([P, 4, 2, W_COLS], BF16, name="w_raw_%d_%d" % (r, kv))
@@ -68,16 +72,14 @@ def tile_linearattention_pa_kernel(tc, x, w_k, w_v, cos_tab, sin_tab, out):
 
         load_weights(0, KEYS)
         load_x(0, 0)
-        load_weights(0, VALUES)
         load_tables(0, 0)
-        load_weights(1, KEYS)
+        load_x(1, 0)
+        load_weights(0, VALUES)
         load_x(0, 1)
         load_tables(0, 1)
-        load_x(1, 0)
         load_x(1, 1)
         for r in range(1, ROUNDS):
-            if r > 1:
-                load_weights(r, KEYS)
+            load_weights(r, KEYS)
             load_tables(r, 0)
             load_tables(r, 1)
             load_weights(r, VALUES)
@@ -93,31 +95,30 @@ def tile_linearattention_pa_kernel(tc, x, w_k, w_v, cos_tab, sin_tab, out):
         x_words = {}
         x_scales = {}
 
-        def quantise_x(b, g):
+        x_grouped = {}
+
+        def turn_x(b, g):
             x_words[b, g] = once.tile([P, PACK, D_PASSES, P], U32, name="x_words_%d_%d" % (b, g), align_bytes=64)
             x_scales[b, g] = once.tile([P, PACK, D_PASSES, P], U8, name="x_scales_%d_%d" % (b, g), align_bytes=64)
-            grouped = {}
             for t in range(PACK):
-                x_f32 = x_raw[b, g, t][:].bitcast(F32)
+                x_f32 = x_raw[b, g, t // 2][:, t % 2, :].bitcast(F32)
                 turned = psum_banks.tile([P, 4, P], F32, name="x_turned", tag="bank")
                 for a in range(4):
                     nc.tensor.transpose(turned[:, a, :], x_f32[:, a * P : (a + 1) * P], identity[:])
-                grouped[t] = four.tile([P, D], BF16, name="x_grouped", align_bytes=64)
+                x_grouped[b, g, t] = four.tile([P, D], BF16, name="x_grouped", align_bytes=64)
                 copy = nc.vector.tensor_copy if (b, g) == (0, 0) and t % 2 == 1 else nc.scalar.copy
                 copy(
-                    out=grouped[t][:].bitcast(F32).rearrange("q (c p u) -> q c p u", c=D_PASSES, u=2),
+                    out=x_grouped[b, g, t][:].bitcast(F32).rearrange("q (c p u) -> q c p u", c=D_PASSES, u=2),
                     in_=turned[:].rearrange("q (c u) p -> q c p u", u=2),
                 )
-                if t > 0:
-                    x_codes(b, g, t - 1, grouped[t - 1])
-            x_codes(b, g, PACK - 1, grouped[PACK - 1])
 
-        def x_codes(b, g, t, grouped):
-            nc.vector.quantize_mx(
-                out=x_words[b, g][:, t, :, :].rearrange("q c p -> q (c p)").bitcast(FP8X4),
-                scales=x_scales[b, g][:, t, :, :].rearrange("q c p -> q (c p)"),
-                in_=grouped[:],
-            )
+        def quantise_x(b, g):
+            for t in range(PACK):
+                nc.vector.quantize_mx(
+                    out=x_words[b, g][:, t, :, :].rearrange("q c p -> q (c p)").bitcast(FP8X4),
+                    scales=x_scales[b, g][:, t, :, :].rearrange("q c p -> q (c p)"),
+                    in_=x_grouped[b, g, t][:],
+                )
 
         w_words = {}
         w_scales = {}
@@ -126,9 +127,11 @@ def tile_linearattention_pa_kernel(tc, x, w_k, w_v, cos_tab, sin_tab, out):
 
         def group_weights(r, kv):
             vector, scalar = nc.vector.tensor_copy, nc.scalar.copy
-            copies = {(0, KEYS): (vector, scalar), (0, VALUES): (vector, vector), (1, KEYS): (vector, vector)}.get(
-                (r, kv), (scalar, scalar)
-            )
+            copies = (scalar, scalar)
+            if (r, kv) == (0, KEYS):
+                copies = (vector, scalar)
+            elif (r, kv) in ((0, VALUES), (1, KEYS)):
+                copies = (vector, vector)
             w_grouped[r, kv] = twice.tile([P, D_PASSES, W_COLS * PACK], BF16, name="w_grouped_%d" % kv, align_bytes=64)
             for c in range(D_PASSES):
                 copies[c](
@@ -174,10 +177,10 @@ def tile_linearattention_pa_kernel(tc, x, w_k, w_v, cos_tab, sin_tab, out):
                     func=ACT.Silu,
                 )
 
-        def rotate_keys(r, b, g):
-            if g == 0:
+        def rotate_keys(r, b, g, heads=range(PAIR)):
+            if (r, b) not in k_rot:
                 k_rot[r, b] = twice.tile([P, N_PASSES, PAIR, 2, DH * PACK], BF16, name="k_rot", align_bytes=64)
-            for hh in range(PAIR):
+            for hh in heads:
                 for s in range(2):
                     nc.vector.tensor_tensor(
                         out=k_rot[r, b][:, g, hh, s, :].rearrange("p (w i t) -> p w t i", t=PACK, i=RUN),
@@ -187,7 +190,7 @@ def tile_linearattention_pa_kernel(tc, x, w_k, w_v, cos_tab, sin_tab, out):
                     )
 
         def values(r, b, g):
-            if g == 0:
+            if (r, b) not in v:
                 v[r, b] = thrice.tile([P, N_PASSES, PAIR, DH * PACK], BF16, name="v", align_bytes=64)
             for hh in range(PAIR):
                 nc.scalar.activation(
@@ -201,13 +204,14 @@ def tile_linearattention_pa_kernel(tc, x, w_k, w_v, cos_tab, sin_tab, out):
         v_words = {}
         v_scales = {}
 
-        def quantise_keys(r, b):
-            k_words[r, b] = thrice.tile([P, N_PASSES, PAIR, 2, DH], U32, name="k_words", align_bytes=64)
-            k_scales[r, b] = thrice.tile([P, N_PASSES, PAIR, 2, DH], U8, name="k_scales", align_bytes=64)
+        def quantise_keys(r, b, passes=slice(0, N_PASSES), heads=slice(0, PAIR)):
+            if (r, b) not in k_words:
+                k_words[r, b] = thrice.tile([P, N_PASSES, PAIR, 2, DH], U32, name="k_words", align_bytes=64)
+                k_scales[r, b] = thrice.tile([P, N_PASSES, PAIR, 2, DH], U8, name="k_scales", align_bytes=64)
             nc.vector.quantize_mx(
-                out=k_words[r, b][:].rearrange("p g h s j -> p (g h s j)").bitcast(FP8X4),
-                scales=k_scales[r, b][:].rearrange("p g h s j -> p (g h s j)"),
-                in_=k_rot[r, b][:].rearrange("p g h s w -> p (g h s w)"),
+                out=k_words[r, b][:, passes, heads, :, :].rearrange("p g h s j -> p (g h s j)").bitcast(FP8X4),
+                scales=k_scales[r, b][:, passes, heads, :, :].rearrange("p g h s j -> p (g h s j)"),
+                in_=k_rot[r, b][:, passes, heads, :, :].rearrange("p g h s w -> p (g h s w)"),
             )
 
         def quantise_values(r, b):
@@ -219,9 +223,9 @@ def tile_linearattention_pa_kernel(tc, x, w_k, w_v, cos_tab, sin_tab, out):
                 in_=v[r, b][:].rearrange("p g h w -> p (g h w)"),
             )
 
-        def state(r, b):
+        def state(r, b, heads=range(PAIR)):
             sums = psum_state.tile([P, PAIR, 2, DH], F32, name="sums")
-            for hh in range(PAIR):
+            for hh in heads:
                 for s in range(2):
                     for g in range(N_PASSES):
                         nc.tensor.matmul_mx(
@@ -234,49 +238,75 @@ def tile_linearattention_pa_kernel(tc, x, w_k, w_v, cos_tab, sin_tab, out):
                             stop=(g == N_PASSES - 1),
                         )
             result = twice.tile([P, PAIR, 2, DH], F32, name="result")
-            nc.scalar.activation(out=result[:], in_=sums[:], func=ACT.Copy, scale=1.0 / 16.0)
+            done = slice(heads[0], heads[-1] + 1)
+            nc.scalar.activation(out=result[:, done, :, :], in_=sums[:, done, :, :], func=ACT.Copy, scale=1.0 / 16.0)
             nc.sync.dma_start(
-                out=out[b, r * PAIR : (r + 1) * PAIR].rearrange("h (s e) d -> e (h s) d", s=2),
-                in_=result[:].rearrange("e h s d -> e (h s) d"),
+                out=out[b, r * PAIR + heads[0] : r * PAIR + heads[-1] + 1].rearrange("h (s e) d -> e (h s) d", s=2),
+                in_=result[:, done, :, :].rearrange("e h s d -> e (h s) d"),
             )
 
-        def want_x(b, g):
-            if (b, g) not in x_words:
-                quantise_x(b, g)
+        def prepare_weights(r, kv):
+            group_weights(r, kv)
+            quantise_weights(r, kv)
 
-        def want_weights(r, kv):
-            if (r, kv) not in w_words:
-                if (r, kv) not in w_grouped:
-                    group_weights(r, kv)
-                quantise_weights(r, kv)
+        prepare_weights(0, KEYS)
+        turn_x(0, 0)
+        quantise_x(0, 0)
+        project_keys(0, 0, 0)
+        rotate_keys(0, 0, 0)
+        turn_x(1, 0)
+        quantise_x(1, 0)
+        project_keys(0, 1, 0)
+        group_weights(0, VALUES)
+        rotate_keys(0, 1, 0)
+        turn_x(0, 1)
+        quantise_x(0, 1)
+        project_keys(0, 0, 1)
+        quantise_weights(0, VALUES)
+        rotate_keys(0, 0, 1)
+        turn_x(1, 1)
+        values(0, 0, 0)
+        quantise_x(1, 1)
+        project_keys(0, 1, 1)
+        prepare_weights(1, KEYS)
+        rotate_keys(0, 1, 1)
+        quantise_keys(0, 0)
+        values(0, 1, 0)
+        group_weights(1, VALUES)
 
+        GROUPED = {2: (2, KEYS), 3: (2, VALUES), 4: (3, KEYS), 5: (3, VALUES)}
+        QUANTISED = {2: (1, VALUES), 3: (2, KEYS), 4: (2, VALUES), 5: (3, KEYS), 6: (3, VALUES)}
         units = [(r, b) for r in range(ROUNDS) for b in range(B)]
-        chunks = [(b, g) for b in range(B) for g in range(N_PASSES)]
-        want_weights(0, KEYS)
-        want_x(0, 0)
-        for i, (r, b) in enumerate(units):
-            next_round = min(r + 1, ROUNDS - 1)
-            for g in range(N_PASSES):
-                if i > 0 or g > 0:
-                    want_x(*chunks[min(chunks.index((b, g)) + 1, len(chunks) - 1)])
-                else:
-                    group_weights(0, VALUES)
-                if (b, g) == (0, 1):
-                    want_weights(next_round, KEYS)
-                project_keys(r, b, g)
-                rotate_keys(r, b, g)
-                want_weights(r, VALUES)
-                if i == 0 and g == 0:
-                    group_weights(1, KEYS)
-                    want_x(0, 1)
-                    quantise_weights(1, KEYS)
-                if (b, g) == (1, 0):
-                    want_weights(next_round, VALUES)
-            quantise_keys(r, b)
-            for g in range(N_PASSES):
-                values(r, b, g)
-            quantise_values(r, b)
-            if i >= STATE_LAG:
-                state(*units[i - STATE_LAG])
-        for r, b in units[-STATE_LAG:]:
-            state(r, b)
+        for i in range(2, len(units)):
+            last = i == len(units) - 1
+            project_keys(*units[i], 0)
+            rotate_keys(*units[i], 0)
+            if i in QUANTISED:
+                quantise_weights(*QUANTISED[i])
+            if i > 2:
+                values(*units[i - 1], 0)
+            quantise_keys(*units[i - 1])
+            project_keys(*units[i], 1)
+            if not last:
+                rotate_keys(*units[i], 1)
+            values(*units[0 if i == 2 else i - 1], 1)
+            quantise_values(*units[i - 2])
+            if i > 2:
+                state(*units[i - 3])
+            if i == 2:
+                values(*units[1], 1)
+            if i in GROUPED:
+                group_weights(*GROUPED[i])
+        r, b = units[-1]
+        for g in range(N_PASSES):
+            values(r, b, g)
+        state(r - 1, b)
+        quantise_values(r, b - 1)
+        rotate_keys(r, b, 1, heads=[0])
+        quantise_keys(r, b, passes=slice(0, 1))
+        state(r, b - 1)
+        quantise_values(r, b)
+        rotate_keys(r, b, 1, heads=[1])
+        for hh in range(PAIR):
+            quantise_keys(r, b, passes=slice(1, 2), heads=slice(hh, hh + 1))
+            state(r, b, heads=[hh])

@@ -21,7 +21,7 @@ PAIR = 2
 ROUNDS = H // PAIR
 W_COLS = PAIR * DH
 KEYS, VALUES = 0, 1
-RUN = 4
+RUN = 2
 STATE_LAG = 2
 
 FLOPS = 2 * B * N * D * 2 * H * DH + 2 * B * H * 2 * DH * DH * N

@@ -52,13 +52,15 @@ def tile_linearattention_pa_kernel(tc, x, w_k, w_v, cos_tab, sin_tab, out):
                 else:
                     nc.sync.dma_start(out=x_raw[b, g, u][:], in_=rows[:, 2 * u : 2 * u + 2, :])
 
-        def load_weights(r, kv):
-            w_raw[r, kv] = once.tile([P, 4, 2, W_COLS], BF16, name="w_raw_%d_%d" % (r, kv))
+        def load_weights(r, kv, halves=(slice(0, 4),)):
+            if (r, kv) not in w_raw:
+                w_raw[r, kv] = once.tile([P, 4, 2, W_COLS], BF16, name="w_raw_%d_%d" % (r, kv))
             rows = (w_k, w_v)[kv].rearrange("(a q e) c -> q a e c", a=4, e=2)
-            for e in range(2):
-                nc.sync.dma_start(
-                    out=w_raw[r, kv][:, :, e, :], in_=rows[:, :, e, r * W_COLS : (r + 1) * W_COLS]
-                )
+            for half in halves:
+                for e in range(2):
+                    nc.sync.dma_start(
+                        out=w_raw[r, kv][:, half, e, :], in_=rows[:, half, e, r * W_COLS : (r + 1) * W_COLS]
+                    )
 
         def load_tables(r, g):
             tables[r, g] = once.tile([P, PAIR, 2, PACK * DH], BF16, name="tables_%d_%d" % (r, g))
@@ -92,6 +94,14 @@ def tile_linearattention_pa_kernel(tc, x, w_k, w_v, cos_tab, sin_tab, out):
         identity = once.tile([P, P], F32)
         masks.make_identity(nc, identity[:])
 
+        zeros = once.tile([P, 512], BF16, align_bytes=64)
+        nc.vector.memset(zeros[:], 0.0)
+
+        def warm_up(times):
+            warm = psum_state.tile([P, 512], F32, name="sums")
+            for i in range(times):
+                nc.tensor.matmul(warm[:], lhsT=zeros[:, 0:P], rhs=zeros[:], start=True, stop=True)
+
         x_words = {}
         x_scales = {}
 
@@ -105,19 +115,24 @@ def tile_linearattention_pa_kernel(tc, x, w_k, w_v, cos_tab, sin_tab, out):
                 turned = psum_banks.tile([P, 4, P], F32, name="x_turned", tag="bank")
                 for a in range(4):
                     nc.tensor.transpose(turned[:, a, :], x_f32[:, a * P : (a + 1) * P], identity[:])
-                x_grouped[b, g, t] = four.tile([P, D], BF16, name="x_grouped", align_bytes=64)
+                if t % 2 == 0:
+                    x_grouped[b, g, t // 2] = thrice.tile([P, 2, D], BF16, name="x_grouped", align_bytes=64)
                 copy = nc.vector.tensor_copy if (b, g) == (0, 0) and t % 2 == 1 else nc.scalar.copy
+                if (b, g) == (0, 0):
+                    warm_up(1 if t < PACK - 1 else 3)
                 copy(
-                    out=x_grouped[b, g, t][:].bitcast(F32).rearrange("q (c p u) -> q c p u", c=D_PASSES, u=2),
+                    out=x_grouped[b, g, t // 2][:, t % 2, :].bitcast(F32).rearrange("q (c p u) -> q c p u", c=D_PASSES, u=2),
                     in_=turned[:].rearrange("q (c u) p -> q c p u", u=2),
                 )
 
+        X_PIECES = ((0, 2), (2, 1), (3, 1))
+
         def quantise_x(b, g):
-            for t in range(PACK):
+            for t, width in X_PIECES:
                 nc.vector.quantize_mx(
-                    out=x_words[b, g][:, t, :, :].rearrange("q c p -> q (c p)").bitcast(FP8X4),
-                    scales=x_scales[b, g][:, t, :, :].rearrange("q c p -> q (c p)"),
-                    in_=x_grouped[b, g, t][:],
+                    out=x_words[b, g][:, t : t + width, :, :].rearrange("q t c p -> q (t c p)").bitcast(FP8X4),
+                    scales=x_scales[b, g][:, t : t + width, :, :].rearrange("q t c p -> q (t c p)"),
+                    in_=x_grouped[b, g, t // 2][:, t % 2 : t % 2 + width, :].rearrange("q t d -> q (t d)"),
                 )
 
         w_words = {}
@@ -237,7 +252,7 @@ def tile_linearattention_pa_kernel(tc, x, w_k, w_v, cos_tab, sin_tab, out):
                             start=(g == 0),
                             stop=(g == N_PASSES - 1),
                         )
-            result = twice.tile([P, PAIR, 2, DH], F32, name="result")
+            result = four.tile([P, PAIR, 2, DH], F32, name="result")
             done = slice(heads[0], heads[-1] + 1)
             nc.scalar.activation(out=result[:, done, :, :], in_=sums[:, done, :, :], func=ACT.Copy, scale=1.0 / 16.0)
             nc.sync.dma_start(
@@ -249,6 +264,7 @@ def tile_linearattention_pa_kernel(tc, x, w_k, w_v, cos_tab, sin_tab, out):
             group_weights(r, kv)
             quantise_weights(r, kv)
 
+        warm_up(8)
         prepare_weights(0, KEYS)
         turn_x(0, 0)
         quantise_x(0, 0)

@@ -83,8 +83,8 @@ def tile_linearattention_pa_kernel(tc, x, w_k, w_v, cos_tab, sin_tab, out):
         for r in range(1, ROUNDS):
             load_weights(r, KEYS)
             load_tables(r, 0)
-            load_tables(r, 1)
             load_weights(r, VALUES)
+            load_tables(r, 1)
 
         table_in = once.tile([P, 1], F32)
         table_out = once.tile([P, 1], F32)
@@ -98,7 +98,7 @@ def tile_linearattention_pa_kernel(tc, x, w_k, w_v, cos_tab, sin_tab, out):
         nc.vector.memset(zeros[:], 0.0)
 
         def warm_up(times):
-            warm = psum_state.tile([P, 512], F32, name="sums")
+            warm = psum_state.tile([P, 512], F32, name="warm", tag="sums")
             for i in range(times):
                 nc.tensor.matmul(warm[:], lhsT=zeros[:, 0:P], rhs=zeros[:], start=True, stop=True)
 
@@ -107,16 +107,13 @@ def tile_linearattention_pa_kernel(tc, x, w_k, w_v, cos_tab, sin_tab, out):
 
         x_grouped = {}
 
-        def turn_x(b, g):
-            x_words[b, g] = once.tile([P, PACK, D_PASSES, P], U32, name="x_words_%d_%d" % (b, g), align_bytes=64)
-            x_scales[b, g] = once.tile([P, PACK, D_PASSES, P], U8, name="x_scales_%d_%d" % (b, g), align_bytes=64)
-            for t in range(PACK):
+        def turn_x(b, g, pair):
+            x_grouped[b, g, pair] = thrice.tile([P, 2, D], BF16, name="x_grouped", align_bytes=64)
+            for t in (2 * pair, 2 * pair + 1):
                 x_f32 = x_raw[b, g, t // 2][:, t % 2, :].bitcast(F32)
                 turned = psum_banks.tile([P, 4, P], F32, name="x_turned", tag="bank")
                 for a in range(4):
                     nc.tensor.transpose(turned[:, a, :], x_f32[:, a * P : (a + 1) * P], identity[:])
-                if t % 2 == 0:
-                    x_grouped[b, g, t // 2] = thrice.tile([P, 2, D], BF16, name="x_grouped", align_bytes=64)
                 copy = nc.vector.tensor_copy if (b, g) == (0, 0) and t % 2 == 1 else nc.scalar.copy
                 if (b, g) == (0, 0):
                     warm_up(1 if t < PACK - 1 else 3)
@@ -125,15 +122,19 @@ def tile_linearattention_pa_kernel(tc, x, w_k, w_v, cos_tab, sin_tab, out):
                     in_=turned[:].rearrange("q (c u) p -> q c p u", u=2),
                 )
 
-        X_PIECES = ((0, 2), (2, 1), (3, 1))
+        def quantise_x(b, g, t, width):
+            if (b, g) not in x_words:
+                x_words[b, g] = once.tile([P, PACK, D_PASSES, P], U32, name="x_words_%d_%d" % (b, g), align_bytes=64)
+                x_scales[b, g] = once.tile([P, PACK, D_PASSES, P], U8, name="x_scales_%d_%d" % (b, g), align_bytes=64)
+            nc.vector.quantize_mx(
+                out=x_words[b, g][:, t : t + width, :, :].rearrange("q t c p -> q (t c p)").bitcast(FP8X4),
+                scales=x_scales[b, g][:, t : t + width, :, :].rearrange("q t c p -> q (t c p)"),
+                in_=x_grouped[b, g, t // 2][:, t % 2 : t % 2 + width, :].rearrange("q t d -> q (t d)"),
+            )
 
-        def quantise_x(b, g):
-            for t, width in X_PIECES:
-                nc.vector.quantize_mx(
-                    out=x_words[b, g][:, t : t + width, :, :].rearrange("q t c p -> q (t c p)").bitcast(FP8X4),
-                    scales=x_scales[b, g][:, t : t + width, :, :].rearrange("q t c p -> q (t c p)"),
-                    in_=x_grouped[b, g, t // 2][:, t % 2 : t % 2 + width, :].rearrange("q t d -> q (t d)"),
-                )
+        def quantise_chunk(b, g):
+            for t, width in ((0, 2), (2, 1), (3, 1)):
+                quantise_x(b, g, t, width)
 
         w_words = {}
         w_scales = {}
@@ -143,9 +144,7 @@ def tile_linearattention_pa_kernel(tc, x, w_k, w_v, cos_tab, sin_tab, out):
         def group_weights(r, kv):
             vector, scalar = nc.vector.tensor_copy, nc.scalar.copy
             copies = (scalar, scalar)
-            if (r, kv) == (0, KEYS):
-                copies = (vector, scalar)
-            elif (r, kv) in ((0, VALUES), (1, KEYS)):
+            if r == 0:
                 copies = (vector, vector)
             w_grouped[r, kv] = twice.tile([P, D_PASSES, W_COLS * PACK], BF16, name="w_grouped_%d" % kv, align_bytes=64)
             for c in range(D_PASSES):
@@ -192,17 +191,17 @@ def tile_linearattention_pa_kernel(tc, x, w_k, w_v, cos_tab, sin_tab, out):
                     func=ACT.Silu,
                 )
 
-        def rotate_keys(r, b, g, heads=range(PAIR)):
+        def rotate_keys(r, b, g, pieces=range(2 * PAIR)):
             if (r, b) not in k_rot:
                 k_rot[r, b] = twice.tile([P, N_PASSES, PAIR, 2, DH * PACK], BF16, name="k_rot", align_bytes=64)
-            for hh in heads:
-                for s in range(2):
-                    nc.vector.tensor_tensor(
-                        out=k_rot[r, b][:, g, hh, s, :].rearrange("p (w i t) -> p w t i", t=PACK, i=RUN),
-                        in0=k[r, b, g][:, hh, :].rearrange("p (w t i) -> p w t i", t=PACK, i=RUN),
-                        in1=tables[r, g][:, hh, s, :].rearrange("p (t w i) -> p w t i", t=PACK, i=RUN),
-                        op=mybir.AluOpType.mult,
-                    )
+            for piece in pieces:
+                hh, s = divmod(piece, 2)
+                nc.vector.tensor_tensor(
+                    out=k_rot[r, b][:, g, hh, s, :].rearrange("p (w i t) -> p w t i", t=PACK, i=RUN),
+                    in0=k[r, b, g][:, hh, :].rearrange("p (w t i) -> p w t i", t=PACK, i=RUN),
+                    in1=tables[r, g][:, hh, s, :].rearrange("p (t w i) -> p w t i", t=PACK, i=RUN),
+                    op=mybir.AluOpType.mult,
+                )
 
         def values(r, b, g):
             if (r, b) not in v:
@@ -219,14 +218,14 @@ def tile_linearattention_pa_kernel(tc, x, w_k, w_v, cos_tab, sin_tab, out):
         v_words = {}
         v_scales = {}
 
-        def quantise_keys(r, b, passes=slice(0, N_PASSES), heads=slice(0, PAIR)):
+        def quantise_keys(r, b, passes=slice(0, N_PASSES), heads=slice(0, PAIR), sides=slice(0, 2)):
             if (r, b) not in k_words:
-                k_words[r, b] = thrice.tile([P, N_PASSES, PAIR, 2, DH], U32, name="k_words", align_bytes=64)
-                k_scales[r, b] = thrice.tile([P, N_PASSES, PAIR, 2, DH], U8, name="k_scales", align_bytes=64)
+                k_words[r, b] = four.tile([P, N_PASSES, PAIR, 2, DH], U32, name="k_words", align_bytes=64)
+                k_scales[r, b] = four.tile([P, N_PASSES, PAIR, 2, DH], U8, name="k_scales", align_bytes=64)
             nc.vector.quantize_mx(
-                out=k_words[r, b][:, passes, heads, :, :].rearrange("p g h s j -> p (g h s j)").bitcast(FP8X4),
-                scales=k_scales[r, b][:, passes, heads, :, :].rearrange("p g h s j -> p (g h s j)"),
-                in_=k_rot[r, b][:, passes, heads, :, :].rearrange("p g h s w -> p (g h s w)"),
+                out=k_words[r, b][:, passes, heads, sides, :].rearrange("p g h s j -> p (g h s j)").bitcast(FP8X4),
+                scales=k_scales[r, b][:, passes, heads, sides, :].rearrange("p g h s j -> p (g h s j)"),
+                in_=k_rot[r, b][:, passes, heads, sides, :].rearrange("p g h s w -> p (g h s w)"),
             )
 
         def quantise_values(r, b):
@@ -238,10 +237,10 @@ def tile_linearattention_pa_kernel(tc, x, w_k, w_v, cos_tab, sin_tab, out):
                 in_=v[r, b][:].rearrange("p g h w -> p (g h w)"),
             )
 
-        def state(r, b, heads=range(PAIR)):
-            sums = psum_state.tile([P, PAIR, 2, DH], F32, name="sums")
-            for hh in heads:
-                for s in range(2):
+        def state(r, b, heads=slice(0, PAIR), sides=slice(0, 2), pool=psum_state, tag="sums"):
+            sums = pool.tile([P, PAIR, 2, DH], F32, name="sums", tag=tag)
+            for hh in range(heads.start, heads.stop):
+                for s in range(sides.start, sides.stop):
                     for g in range(N_PASSES):
                         nc.tensor.matmul_mx(
                             out=sums[:, hh, s, :],
@@ -252,47 +251,61 @@ def tile_linearattention_pa_kernel(tc, x, w_k, w_v, cos_tab, sin_tab, out):
                             start=(g == 0),
                             stop=(g == N_PASSES - 1),
                         )
-            result = four.tile([P, PAIR, 2, DH], F32, name="result")
-            done = slice(heads[0], heads[-1] + 1)
-            nc.scalar.activation(out=result[:, done, :, :], in_=sums[:, done, :, :], func=ACT.Copy, scale=1.0 / 16.0)
+            if pool is psum_state:
+                result = four.tile([P, PAIR, 2, DH], F32, name="result")
+            else:
+                result = once.tile([P, PAIR, 2, DH], F32, name="result_%d" % sides.start)
+            nc.scalar.activation(
+                out=result[:, heads, sides, :], in_=sums[:, heads, sides, :], func=ACT.Copy, scale=1.0 / 16.0
+            )
+            rows = slice(sides.start * P, sides.stop * P)
             nc.sync.dma_start(
-                out=out[b, r * PAIR + heads[0] : r * PAIR + heads[-1] + 1].rearrange("h (s e) d -> e (h s) d", s=2),
-                in_=result[:, done, :, :].rearrange("e h s d -> e (h s) d"),
+                out=out[b, r * PAIR + heads.start : r * PAIR + heads.stop, rows, :].rearrange(
+                    "h (s e) d -> e (h s) d", e=P
+                ),
+                in_=result[:, heads, sides, :].rearrange("e h s d -> e (h s) d"),
             )
 
-        def prepare_weights(r, kv):
-            group_weights(r, kv)
-            quantise_weights(r, kv)
-
         warm_up(8)
-        prepare_weights(0, KEYS)
-        turn_x(0, 0)
-        quantise_x(0, 0)
+        group_weights(0, KEYS)
+        quantise_weights(0, KEYS)
+        turn_x(0, 0, 0)
+        quantise_x(0, 0, 0, 2)
+        turn_x(0, 0, 1)
+        quantise_x(0, 0, 2, 1)
+        quantise_x(0, 0, 3, 1)
         project_keys(0, 0, 0)
-        rotate_keys(0, 0, 0)
-        turn_x(1, 0)
-        quantise_x(1, 0)
+        rotate_keys(0, 0, 0, range(0, 4))
+        turn_x(1, 0, 0)
+        turn_x(1, 0, 1)
+        quantise_chunk(1, 0)
+        rotate_keys(0, 0, 0, range(4, 4))
         project_keys(0, 1, 0)
         group_weights(0, VALUES)
-        rotate_keys(0, 1, 0)
-        turn_x(0, 1)
-        quantise_x(0, 1)
-        project_keys(0, 0, 1)
         quantise_weights(0, VALUES)
-        rotate_keys(0, 0, 1)
-        turn_x(1, 1)
+        rotate_keys(0, 1, 0, range(0, 3))
+        turn_x(0, 1, 0)
+        turn_x(0, 1, 1)
         values(0, 0, 0)
-        quantise_x(1, 1)
+        quantise_chunk(0, 1)
+        rotate_keys(0, 1, 0, range(3, 4))
+        project_keys(0, 0, 1)
+        rotate_keys(0, 0, 1, range(0, 3))
+        turn_x(1, 1, 0)
+        turn_x(1, 1, 1)
+        group_weights(1, KEYS)
+        quantise_chunk(1, 1)
+        rotate_keys(0, 0, 1, range(3, 4))
         project_keys(0, 1, 1)
-        prepare_weights(1, KEYS)
-        rotate_keys(0, 1, 1)
         quantise_keys(0, 0)
-        values(0, 1, 0)
+        quantise_weights(1, KEYS)
+        rotate_keys(0, 1, 1)
         group_weights(1, VALUES)
 
         GROUPED = {2: (2, KEYS), 3: (2, VALUES), 4: (3, KEYS), 5: (3, VALUES)}
         QUANTISED = {2: (1, VALUES), 3: (2, KEYS), 4: (2, VALUES), 5: (3, KEYS), 6: (3, VALUES)}
         units = [(r, b) for r in range(ROUNDS) for b in range(B)]
+        waiting = [(0, 1, 0), (0, 0, 1), (0, 1, 1)] + [(r, b, g) for r, b in units[2:] for g in range(N_PASSES)]
         for i in range(2, len(units)):
             last = i == len(units) - 1
             project_keys(*units[i], 0)
@@ -300,29 +313,32 @@ def tile_linearattention_pa_kernel(tc, x, w_k, w_v, cos_tab, sin_tab, out):
             if i in QUANTISED:
                 quantise_weights(*QUANTISED[i])
             if i > 2:
-                values(*units[i - 1], 0)
+                values(*waiting[2 * (i - 2) - 1])
             quantise_keys(*units[i - 1])
             project_keys(*units[i], 1)
+            if i >= 3:
+                quantise_values(*units[i - 3])
             if not last:
                 rotate_keys(*units[i], 1)
-            values(*units[0 if i == 2 else i - 1], 1)
-            quantise_values(*units[i - 2])
-            if i > 2:
-                state(*units[i - 3])
-            if i == 2:
-                values(*units[1], 1)
+            values(*waiting[2 * (i - 2)])
+            if i >= 4:
+                state(*units[i - 4])
             if i in GROUPED:
                 group_weights(*GROUPED[i])
         r, b = units[-1]
-        for g in range(N_PASSES):
-            values(r, b, g)
-        state(r - 1, b)
-        quantise_values(r, b - 1)
-        rotate_keys(r, b, 1, heads=[0])
+        for chunk in waiting[-4:]:
+            values(*chunk)
+        state(*units[4])
+        quantise_values(*units[5])
+        rotate_keys(r, b, 1, range(0, 2))
+        state(*units[5])
+        quantise_values(*units[6])
         quantise_keys(r, b, passes=slice(0, 1))
-        state(r, b - 1)
-        quantise_values(r, b)
-        rotate_keys(r, b, 1, heads=[1])
-        for hh in range(PAIR):
-            quantise_keys(r, b, passes=slice(1, 2), heads=slice(hh, hh + 1))
-            state(r, b, heads=[hh])
+        state(*units[6])
+        rotate_keys(r, b, 1, range(2, 4))
+        quantise_values(*units[7])
+        quantise_keys(r, b, passes=slice(1, 2), heads=slice(0, 1))
+        state(r, b, heads=slice(0, 1))
+        for s in range(2):
+            quantise_keys(r, b, passes=slice(1, 2), heads=slice(1, 2), sides=slice(s, s + 1))
+            state(r, b, heads=slice(1, 2), sides=slice(s, s + 1), pool=psum_banks, tag="bank")

@@ -132,6 +132,13 @@ def tile_linearattention_pa_kernel(tc, x, w_k, w_v, cos_tab, sin_tab, out):
                 in_=x_grouped[b, g, t // 2][:, t % 2 : t % 2 + width, :].rearrange("q t d -> q (t d)"),
             )
 
+        def stay_warm(b, g):
+            warm = psum_state.tile([P, 512], F32, name="warm", tag="sums")
+            for t in range(PACK - 1):
+                nc.tensor.matmul(
+                    warm[:], lhsT=zeros[:, 0:P], rhs=x_grouped[b, g, t // 2][:, t % 2, 0:512], start=True, stop=True
+                )
+
         def quantise_chunk(b, g):
             for t, width in ((0, 2), (2, 1), (3, 1)):
                 quantise_x(b, g, t, width)
@@ -280,6 +287,7 @@ def tile_linearattention_pa_kernel(tc, x, w_k, w_v, cos_tab, sin_tab, out):
         turn_x(1, 0, 1)
         quantise_chunk(1, 0)
         rotate_keys(0, 0, 0, range(4, 4))
+        stay_warm(1, 0)
         project_keys(0, 1, 0)
         group_weights(0, VALUES)
         quantise_weights(0, VALUES)
@@ -296,6 +304,7 @@ def tile_linearattention_pa_kernel(tc, x, w_k, w_v, cos_tab, sin_tab, out):
         group_weights(1, KEYS)
         quantise_chunk(1, 1)
         rotate_keys(0, 0, 1, range(3, 4))
+        stay_warm(1, 1)
         project_keys(0, 1, 1)
         quantise_keys(0, 0)
         quantise_weights(1, KEYS)

@@ -52,15 +52,12 @@ def tile_linearattention_pa_kernel(tc, x, w_k, w_v, cos_tab, sin_tab, out):
                 else:
                     nc.sync.dma_start(out=x_raw[b, g, u][:], in_=rows[:, 2 * u : 2 * u + 2, :])
 
-        def load_weights(r, kv, halves=(slice(0, 4),)):
-            if (r, kv) not in w_raw:
-                w_raw[r, kv] = once.tile([P, 4, 2, W_COLS], BF16, name="w_raw_%d_%d" % (r, kv))
+        def load_weights(r, kv, first=0, heads=PAIR):
+            w_raw[r, kv, first] = once.tile([P, 4, 2, heads * DH], BF16, name="w_raw_%d_%d_%d" % (r, kv, first))
             rows = (w_k, w_v)[kv].rearrange("(a q e) c -> q a e c", a=4, e=2)
-            for half in halves:
-                for e in range(2):
-                    nc.sync.dma_start(
-                        out=w_raw[r, kv][:, half, e, :], in_=rows[:, half, e, r * W_COLS : (r + 1) * W_COLS]
-                    )
+            start = r * W_COLS + first * DH
+            for e in range(2):
+                nc.sync.dma_start(out=w_raw[r, kv, first][:, :, e, :], in_=rows[:, :, e, start : start + heads * DH])
 
         def load_tables(r, g):
             tables[r, g] = once.tile([P, PAIR, 2, PACK * DH], BF16, name="tables_%d_%d" % (r, g))
@@ -72,8 +69,9 @@ def tile_linearattention_pa_kernel(tc, x, w_k, w_v, cos_tab, sin_tab, out):
                     ),
                 )
 
-        load_weights(0, KEYS)
+        load_weights(0, KEYS, first=0, heads=1)
         load_x(0, 0)
+        load_weights(0, KEYS, first=1, heads=1)
         load_tables(0, 0)
         load_x(1, 0)
         load_weights(0, VALUES)
@@ -148,38 +146,43 @@ def tile_linearattention_pa_kernel(tc, x, w_k, w_v, cos_tab, sin_tab, out):
 
         w_grouped = {}
 
-        def group_weights(r, kv):
-            vector, scalar = nc.vector.tensor_copy, nc.scalar.copy
-            copies = (scalar, scalar)
-            if r == 0:
-                copies = (vector, vector)
-            w_grouped[r, kv] = twice.tile([P, D_PASSES, W_COLS * PACK], BF16, name="w_grouped_%d" % kv, align_bytes=64)
+        def group_weights(r, kv, first=0, heads=PAIR):
+            copy = nc.vector.tensor_copy if r == 0 and first == 0 else nc.scalar.copy
+            grouped = once.tile(
+                [P, D_PASSES, heads * DH * PACK], BF16, name="w_grouped", tag="w_grouped_%d_%d_%d" % (kv, heads, first), align_bytes=64
+            )
+            w_grouped[r, kv, first] = grouped
             for c in range(D_PASSES):
-                copies[c](
-                    out=w_grouped[r, kv][:, c, :].rearrange("q (w i t) -> q w t i", i=4, t=PACK),
-                    in_=w_raw[r, kv][:, 2 * c : 2 * c + 2, :, :].rearrange("q u e (w i) -> q w (u e) i", i=4),
+                copy(
+                    out=grouped[:, c, :].rearrange("q (w i t) -> q w t i", i=4, t=PACK),
+                    in_=w_raw[r, kv, first][:, 2 * c : 2 * c + 2, :, :].rearrange("q u e (w i) -> q w (u e) i", i=4),
                 )
 
-        def quantise_weights(r, kv):
-            w_words[r, kv] = twice.tile([P, D_PASSES, W_COLS], U32, name="w_words_%d" % kv, align_bytes=64)
-            w_scales[r, kv] = twice.tile([P, D_PASSES, W_COLS], U8, name="w_scales_%d" % kv, align_bytes=64)
+        def quantise_weights(r, kv, first=0, heads=PAIR):
+            pool = once if heads == 1 else twice
+            key = "%d_%d_%d" % (kv, heads, first)
+            words = pool.tile([P, D_PASSES, heads * DH], U32, name="w_words", tag="w_words_" + key, align_bytes=64)
+            scales = pool.tile([P, D_PASSES, heads * DH], U8, name="w_scales", tag="w_scales_" + key, align_bytes=64)
             nc.vector.quantize_mx(
-                out=w_words[r, kv][:].rearrange("q c w -> q (c w)").bitcast(FP8X4),
-                scales=w_scales[r, kv][:].rearrange("q c w -> q (c w)"),
-                in_=w_grouped[r, kv][:].rearrange("q c w -> q (c w)"),
+                out=words[:].rearrange("q c w -> q (c w)").bitcast(FP8X4),
+                scales=scales[:].rearrange("q c w -> q (c w)"),
+                in_=w_grouped[r, kv, first][:].rearrange("q c w -> q (c w)"),
             )
+            for hh in range(heads):
+                cols = slice(hh * DH, (hh + 1) * DH)
+                w_words[r, kv, first + hh] = words[:, :, cols]
+                w_scales[r, kv, first + hh] = scales[:, :, cols]
 
         def project(r, b, g, kv, hh):
             bank = psum_banks.tile([P, PACK, DH], F32, name="kv_bank", tag="bank")
-            cols = slice(hh * DH, (hh + 1) * DH)
             for t in range(PACK):
                 for c in range(D_PASSES):
                     nc.tensor.matmul_mx(
                         out=bank[:, t, :],
                         lhsT=x_words[b, g][:, t, c, :].bitcast(FP8X4),
                         lhsT_scale=x_scales[b, g][:, t, c, :],
-                        rhs=w_words[r, kv][:, c, cols].bitcast(FP8X4),
-                        rhs_scale=w_scales[r, kv][:, c, cols],
+                        rhs=w_words[r, kv, hh][:, c, :].bitcast(FP8X4),
+                        rhs_scale=w_scales[r, kv, hh][:, c, :],
                         start=(c == 0),
                         stop=(c == D_PASSES - 1),
                     )
@@ -274,19 +277,20 @@ def tile_linearattention_pa_kernel(tc, x, w_k, w_v, cos_tab, sin_tab, out):
             )
 
         warm_up(8)
-        group_weights(0, KEYS)
-        quantise_weights(0, KEYS)
+        group_weights(0, KEYS, first=0, heads=1)
+        quantise_weights(0, KEYS, first=0, heads=1)
         turn_x(0, 0, 0)
         quantise_x(0, 0, 0, 2)
         turn_x(0, 0, 1)
+        group_weights(0, KEYS, first=1, heads=1)
         quantise_x(0, 0, 2, 1)
         quantise_x(0, 0, 3, 1)
+        quantise_weights(0, KEYS, first=1, heads=1)
         project_keys(0, 0, 0)
-        rotate_keys(0, 0, 0, range(0, 4))
+        rotate_keys(0, 0, 0)
         turn_x(1, 0, 0)
         turn_x(1, 0, 1)
         quantise_chunk(1, 0)
-        rotate_keys(0, 0, 0, range(4, 4))
         stay_warm(1, 0)
         project_keys(0, 1, 0)
         group_weights(0, VALUES)

from contextlib import ExitStack

import concourse.masks as masks
import concourse.mybir as mybir

BF16 = mybir.dt.bfloat16
F32 = mybir.dt.float32
U32 = mybir.dt.uint32
U8 = mybir.dt.uint8
FP8X4 = mybir.dt.float8_e4m3fn_x4
ACT = mybir.ActivationFunctionType

P = 128
PACK = 4
K_PASS = P * PACK

B, N, D, H, DH = 2, 1024, 1024, 8, 128
D_PASSES = D // K_PASS
N_PASSES = N // K_PASS
PAIR = 2
ROUNDS = H // PAIR
W_COLS = PAIR * DH
KEYS, VALUES = 0, 1
RUN = 2
STATE_LAG = 2

FLOPS = 2 * B * N * D * 2 * H * DH + 2 * B * H * 2 * DH * DH * N


def tile_linearattention_pa_kernel(tc, x, w_k, w_v, cos_tab, sin_tab, out):
    nc = tc.nc
    with ExitStack() as ctx:
        ctx.enter_context(tc.manual_schedule())
        once = ctx.enter_context(tc.tile_pool(name="once", bufs=1))
        twice = ctx.enter_context(tc.tile_pool(name="twice", bufs=2))
        thrice = ctx.enter_context(tc.tile_pool(name="thrice", bufs=3))
        four = ctx.enter_context(tc.tile_pool(name="four", bufs=4))
        psum_banks = ctx.enter_context(tc.psum_pool(name="psum_banks", bufs=6))
        psum_state = ctx.enter_context(tc.psum_pool(name="psum_state", bufs=2))

        x_raw = {}
        w_raw = {}
        tables = {}

        def load_x(b, g):
            rows = x[b, g * K_PASS : (g + 1) * K_PASS, :].rearrange("(p t) d -> p t d", t=PACK)
            for u in range(2):
                x_raw[b, g, u] = once.tile([P, 2, D], BF16, name="x_raw_%d_%d_%d" % (b, g, u))
                if (b, g) == (0, 0):
                    for t in range(2):
                        nc.sync.dma_start(out=x_raw[b, g, u][:, t, :], in_=rows[:, 2 * u + t, :])
                else:
                    nc.sync.dma_start(out=x_raw[b, g, u][:], in_=rows[:, 2 * u : 2 * u + 2, :])

        def load_weights(r, kv, first=0, heads=PAIR):
            w_raw[r, kv, first] = once.tile([P, 4, 2, heads * DH], BF16, name="w_raw_%d_%d_%d" % (r, kv, first))
            rows = (w_k, w_v)[kv].rearrange("(a q e) c -> q a e c", a=4, e=2)
            start = r * W_COLS + first * DH
            for e in range(2):
                nc.sync.dma_start(out=w_raw[r, kv, first][:, :, e, :], in_=rows[:, :, e, start : start + heads * DH])

        def load_tables(r, g):
            tables[r, g] = once.tile([P, PAIR, 2, PACK * DH], BF16, name="tables_%d_%d" % (r, g))
            for s, table in enumerate((cos_tab, sin_tab)):
                nc.sync.dma_start(
                    out=tables[r, g][:, :, s, :],
                    in_=table[r * PAIR : (r + 1) * PAIR, g * K_PASS : (g + 1) * K_PASS, :].rearrange(
                        "h (p t) j -> p h (t j)", t=PACK
                    ),
                )

        load_weights(0, KEYS, first=0, heads=1)
        load_x(0, 0)
        load_weights(0, KEYS, first=1, heads=1)
        load_tables(0, 0)
        load_x(1, 0)
        load_weights(0, VALUES)
        load_x(0, 1)
        load_tables(0, 1)
        load_x(1, 1)
        for r in range(1, ROUNDS):
            load_weights(r, KEYS)
            load_tables(r, 0)
            load_weights(r, VALUES)
            load_tables(r, 1)

        table_in = once.tile([P, 1], F32)
        table_out = once.tile([P, 1], F32)
        nc.vector.memset(table_in[:], 0.0)
        nc.scalar.activation(out=table_out[:], in_=table_in[:], func=ACT.Silu)

        identity = once.tile([P, P], F32)
        masks.make_identity(nc, identity[:])

        zeros = once.tile([P, 512], BF16, align_bytes=64)
        nc.vector.memset(zeros[:], 0.0)

        def warm_up(times):
            warm = psum_state.tile([P, 512], F32, name="warm", tag="sums")
            for i in range(times):
                nc.tensor.matmul(warm[:], lhsT=zeros[:, 0:P], rhs=zeros[:], start=True, stop=True)

        x_words = {}
        x_scales = {}

        x_grouped = {}

        def turn_x(b, g, pair):
            x_grouped[b, g, pair] = thrice.tile([P, 2, D], BF16, name="x_grouped", align_bytes=64)
            for t in (2 * pair, 2 * pair + 1):
                x_f32 = x_raw[b, g, t // 2][:, t % 2, :].bitcast(F32)
                turned = psum_banks.tile([P, 4, P], F32, name="x_turned", tag="bank")
                for a in range(4):
                    nc.tensor.transpose(turned[:, a, :], x_f32[:, a * P : (a + 1) * P], identity[:])
                copy = nc.vector.tensor_copy if (b, g) == (0, 0) and t % 2 == 1 else nc.scalar.copy
                if (b, g) == (0, 0):
                    warm_up(1 if t < PACK - 1 else 3)
                copy(
                    out=x_grouped[b, g, t // 2][:, t % 2, :].bitcast(F32).rearrange("q (c p u) -> q c p u", c=D_PASSES, u=2),
                    in_=turned[:].rearrange("q (c u) p -> q c p u", u=2),
                )

        def quantise_x(b, g, t, width):
            if (b, g) not in x_words:
                x_words[b, g] = once.tile([P, PACK, D_PASSES, P], U32, name="x_words_%d_%d" % (b, g), align_bytes=64)
                x_scales[b, g] = once.tile([P, PACK, D_PASSES, P], U8, name="x_scales_%d_%d" % (b, g), align_bytes=64)
            nc.vector.quantize_mx(
                out=x_words[b, g][:, t : t + width, :, :].rearrange("q t c p -> q (t c p)").bitcast(FP8X4),
                scales=x_scales[b, g][:, t : t + width, :, :].rearrange("q t c p -> q (t c p)"),
                in_=x_grouped[b, g, t // 2][:, t % 2 : t % 2 + width, :].rearrange("q t d -> q (t d)"),
            )

        def stay_warm(b, g):
            warm = psum_state.tile([P, 512], F32, name="warm", tag="sums")
            for t in range(PACK - 1):
                nc.tensor.matmul(
                    warm[:], lhsT=zeros[:, 0:P], rhs=x_grouped[b, g, t // 2][:, t % 2, 0:512], start=True, stop=True
                )

        def quantise_chunk(b, g):
            for t, width in ((0, 2), (2, 1), (3, 1)):
                quantise_x(b, g, t, width)

        w_words = {}
        w_scales = {}

        w_grouped = {}

        def group_weights(r, kv, first=0, heads=PAIR):
            copy = nc.vector.tensor_copy if r == 0 and first == 0 else nc.scalar.copy
            grouped = once.tile(
                [P, D_PASSES, heads * DH * PACK], BF16, name="w_grouped", tag="w_grouped_%d_%d_%d" % (kv, heads, first), align_bytes=64
            )
            w_grouped[r, kv, first] = grouped
            for c in range(D_PASSES):
                copy(
                    out=grouped[:, c, :].rearrange("q (w i t) -> q w t i", i=4, t=PACK),
                    in_=w_raw[r, kv, first][:, 2 * c : 2 * c + 2, :, :].rearrange("q u e (w i) -> q w (u e) i", i=4),
                )

        def quantise_weights(r, kv, first=0, heads=PAIR):
            pool = once if heads == 1 else twice
            key = "%d_%d_%d" % (kv, heads, first)
            words = pool.tile([P, D_PASSES, heads * DH], U32, name="w_words", tag="w_words_" + key, align_bytes=64)
            scales = pool.tile([P, D_PASSES, heads * DH], U8, name="w_scales", tag="w_scales_" + key, align_bytes=64)
            nc.vector.quantize_mx(
                out=words[:].rearrange("q c w -> q (c w)").bitcast(FP8X4),
                scales=scales[:].rearrange("q c w -> q (c w)"),
                in_=w_grouped[r, kv, first][:].rearrange("q c w -> q (c w)"),
            )
            for hh in range(heads):
                cols = slice(hh * DH, (hh + 1) * DH)
                w_words[r, kv, first + hh] = words[:, :, cols]
                w_scales[r, kv, first + hh] = scales[:, :, cols]

        def project(r, b, g, kv, hh):
            bank = psum_banks.tile([P, PACK, DH], F32, name="kv_bank", tag="bank")
            for t in range(PACK):
                for c in range(D_PASSES):
                    nc.tensor.matmul_mx(
                        out=bank[:, t, :],
                        lhsT=x_words[b, g][:, t, c, :].bitcast(FP8X4),
                        lhsT_scale=x_scales[b, g][:, t, c, :],
                        rhs=w_words[r, kv, hh][:, c, :].bitcast(FP8X4),
                        rhs_scale=w_scales[r, kv, hh][:, c, :],
                        start=(c == 0),
                        stop=(c == D_PASSES - 1),
                    )
            return bank[:]

        k = {}
        k_rot = {}
        v = {}

        def project_keys(r, b, g):
            k[r, b, g] = four.tile([P, PAIR, DH * PACK], F32, name="k")
            for hh in range(PAIR):
                nc.scalar.activation(
                    out=k[r, b, g][:, hh, :].rearrange("p (w t i) -> p w t i", t=PACK, i=RUN),
                    in_=project(r, b, g, KEYS, hh).rearrange("p t (w i) -> p w t i", i=RUN),
                    func=ACT.Silu,
                )

        def rotate_keys(r, b, g, pieces=range(2 * PAIR)):
            if (r, b) not in k_rot:
                k_rot[r, b] = twice.tile([P, N_PASSES, PAIR, 2, DH * PACK], BF16, name="k_rot", align_bytes=64)
            for piece in pieces:
                hh, s = divmod(piece, 2)
                nc.vector.tensor_tensor(
                    out=k_rot[r, b][:, g, hh, s, :].rearrange("p (w i t) -> p w t i", t=PACK, i=RUN),
                    in0=k[r, b, g][:, hh, :].rearrange("p (w t i) -> p w t i", t=PACK, i=RUN),
                    in1=tables[r, g][:, hh, s, :].rearrange("p (t w i) -> p w t i", t=PACK, i=RUN),
                    op=mybir.AluOpType.mult,
                )

        def values(r, b, g):
            if (r, b) not in v:
                v[r, b] = thrice.tile([P, N_PASSES, PAIR, DH * PACK], BF16, name="v", align_bytes=64)
            for hh in range(PAIR):
                nc.scalar.activation(
                    out=v[r, b][:, g, hh, :].rearrange("p (j t) -> p j t", t=PACK),
                    in_=project(r, b, g, VALUES, hh).rearrange("p t j -> p j t"),
                    func=ACT.Silu,
                )

        k_words = {}
        k_scales = {}
        v_words = {}
        v_scales = {}

        def quantise_keys(r, b, passes=slice(0, N_PASSES), heads=slice(0, PAIR), sides=slice(0, 2)):
            if (r, b) not in k_words:
                k_words[r, b] = four.tile([P, N_PASSES, PAIR, 2, DH], U32, name="k_words", align_bytes=64)
                k_scales[r, b] = four.tile([P, N_PASSES, PAIR, 2, DH], U8, name="k_scales", align_bytes=64)
            nc.vector.quantize_mx(
                out=k_words[r, b][:, passes, heads, sides, :].rearrange("p g h s j -> p (g h s j)").bitcast(FP8X4),
                scales=k_scales[r, b][:, passes, heads, sides, :].rearrange("p g h s j -> p (g h s j)"),
                in_=k_rot[r, b][:, passes, heads, sides, :].rearrange("p g h s w -> p (g h s w)"),
            )

        def quantise_values(r, b):
            v_words[r, b] = thrice.tile([P, N_PASSES, PAIR, DH], U32, name="v_words", align_bytes=64)
            v_scales[r, b] = thrice.tile([P, N_PASSES, PAIR, DH], U8, name="v_scales", align_bytes=64)
            nc.vector.quantize_mx(
                out=v_words[r, b][:].rearrange("p g h j -> p (g h j)").bitcast(FP8X4),
                scales=v_scales[r, b][:].rearrange("p g h j -> p (g h j)"),
                in_=v[r, b][:].rearrange("p g h w -> p (g h w)"),
            )

        def state(r, b, heads=slice(0, PAIR), sides=slice(0, 2), pool=psum_state, tag="sums"):
            sums = pool.tile([P, PAIR, 2, DH], F32, name="sums", tag=tag)
            for hh in range(heads.start, heads.stop):
                for s in range(sides.start, sides.stop):
                    for g in range(N_PASSES):
                        nc.tensor.matmul_mx(
                            out=sums[:, hh, s, :],
                            lhsT=k_words[r, b][:, g, hh, s, :].bitcast(FP8X4),
                            lhsT_scale=k_scales[r, b][:, g, hh, s, :],
                            rhs=v_words[r, b][:, g, hh, :].bitcast(FP8X4),
                            rhs_scale=v_scales[r, b][:, g, hh, :],
                            start=(g == 0),
                            stop=(g == N_PASSES - 1),
                        )
            if pool is psum_state:
                result = four.tile([P, PAIR, 2, DH], F32, name="result")
            else:
                result = once.tile([P, PAIR, 2, DH], F32, name="result_%d" % sides.start)
            nc.scalar.activation(
                out=result[:, heads, sides, :], in_=sums[:, heads, sides, :], func=ACT.Copy, scale=1.0 / 16.0
            )
            rows = slice(sides.start * P, sides.stop * P)
            nc.sync.dma_start(
                out=out[b, r * PAIR + heads.start : r * PAIR + heads.stop, rows, :].rearrange(
                    "h (s e) d -> e (h s) d", e=P
                ),
                in_=result[:, heads, sides, :].rearrange("e h s d -> e (h s) d"),
            )

        warm_up(8)
        group_weights(0, KEYS, first=0, heads=1)
        quantise_weights(0, KEYS, first=0, heads=1)
        turn_x(0, 0, 0)
        quantise_x(0, 0, 0, 2)
        turn_x(0, 0, 1)
        group_weights(0, KEYS, first=1, heads=1)
        quantise_x(0, 0, 2, 1)
        quantise_x(0, 0, 3, 1)
        quantise_weights(0, KEYS, first=1, heads=1)
        project_keys(0, 0, 0)
        rotate_keys(0, 0, 0)
        turn_x(1, 0, 0)
        turn_x(1, 0, 1)
        quantise_chunk(1, 0)
        stay_warm(1, 0)
        project_keys(0, 1, 0)
        group_weights(0, VALUES)
        quantise_weights(0, VALUES)
        rotate_keys(0, 1, 0, range(0, 3))
        turn_x(0, 1, 0)
        turn_x(0, 1, 1)
        values(0, 0, 0)
        quantise_chunk(0, 1)
        rotate_keys(0, 1, 0, range(3, 4))
        project_keys(0, 0, 1)
        rotate_keys(0, 0, 1, range(0, 3))
        turn_x(1, 1, 0)
        turn_x(1, 1, 1)
        group_weights(1, KEYS)
        quantise_chunk(1, 1)
        rotate_keys(0, 0, 1, range(3, 4))
        stay_warm(1, 1)
        project_keys(0, 1, 1)
        quantise_keys(0, 0)
        quantise_weights(1, KEYS)
        rotate_keys(0, 1, 1)
        group_weights(1, VALUES)

        GROUPED = {2: (2, KEYS), 3: (2, VALUES), 4: (3, KEYS), 5: (3, VALUES)}
        QUANTISED = {2: (1, VALUES), 3: (2, KEYS), 4: (2, VALUES), 5: (3, KEYS), 6: (3, VALUES)}
        units = [(r, b) for r in range(ROUNDS) for b in range(B)]
        waiting = [(0, 1, 0), (0, 0, 1), (0, 1, 1)] + [(r, b, g) for r, b in units[2:] for g in range(N_PASSES)]
        for i in range(2, len(units)):
            last = i == len(units) - 1
            project_keys(*units[i], 0)
            rotate_keys(*units[i], 0)
            if i in QUANTISED:
                quantise_weights(*QUANTISED[i])
            if i > 2:
                values(*waiting[2 * (i - 2) - 1])
            quantise_keys(*units[i - 1])
            project_keys(*units[i], 1)
            if i >= 3:
                quantise_values(*units[i - 3])
            if not last:
                rotate_keys(*units[i], 1)
            values(*waiting[2 * (i - 2)])
            if i >= 4:
                state(*units[i - 4])
            if i in GROUPED:
                group_weights(*GROUPED[i])
        r, b = units[-1]
        for chunk in waiting[-4:]:
            values(*chunk)
        state(*units[4])
        quantise_values(*units[5])
        rotate_keys(r, b, 1, range(0, 2))
        state(*units[5])
        quantise_values(*units[6])
        quantise_keys(r, b, passes=slice(0, 1))
        state(*units[6])
        rotate_keys(r, b, 1, range(2, 4))
        quantise_values(*units[7])
        quantise_keys(r, b, passes=slice(1, 2), heads=slice(0, 1))
        state(r, b, heads=slice(0, 1))
        for s in range(2):
            quantise_keys(r, b, passes=slice(1, 2), heads=slice(1, 2), sides=slice(s, s + 1))
            state(r, b, heads=slice(1, 2), sides=slice(s, s + 1), pool=psum_banks, tag="bank")
